import numpy as np
import ml_dtypes


def mxq(x, axis, fmt="e4m3"):
    dtype, down = {"e4m3": (ml_dtypes.float8_e4m3fn, 7), "e5m2": (ml_dtypes.float8_e5m2, 14)}[fmt]
    v = np.moveaxis(np.asarray(x, np.float32).astype(ml_dtypes.bfloat16).astype(np.float64), axis, -1)
    blocks = v.reshape(v.shape[:-1] + (-1, 32))
    amax = np.abs(blocks).max(-1, keepdims=True)
    byte = np.maximum(np.where(amax > 0, np.frexp(amax)[1] - 1 + 127, 0) - down, 1)
    scale = np.exp2(byte - 127.0)
    codes = (blocks / scale).astype(np.float32).astype(dtype).astype(np.float64)
    return np.moveaxis((codes * scale).reshape(v.shape), -1, axis)


WIDE = False


def mx_kscale(k):
    if not WIDE:
        return np.ones(k)
    levels = np.array([10, -10, 5, -5, 0])
    a = np.random.permutation(np.resize(levels, k // 512 * 4)).reshape(k // 512, 4)
    idx = np.arange(k)
    return np.exp2(a[idx // 512, idx % 128 // 32])


BF16 = ml_dtypes.bfloat16


def bf(x):
    return np.asarray(x, np.float32).astype(BF16)


def f64(x):
    return np.asarray(x).astype(np.float64)


G, S, M, H, E, C = 2, 512, 512, 1024, 16, 64


def setup_inputs():
    t = mx_kscale(H)
    u = mx_kscale(E * C).reshape(E, C)
    return {"h": bf(np.maximum(np.random.standard_normal((E, G, C, H)), 0.0) * 1.4 * t * u[:, None, :, None]),
            "wo": bf(np.random.standard_normal((E, H, M)) * 10.0 / np.sqrt(H * E * C) / t[None, :, None]),
            "combined_weights": bf(np.random.standard_normal((G, S, E, C)) * 0.1 / u)}


def reference(h, wo, combined_weights):
    eo = mxq(f64(h).reshape(E, G * C, H), 2, "e4m3") @ mxq(f64(wo), 1, "e4m3")
    expert_outputs = eo.reshape(E, G, C, M).transpose(1, 0, 2, 3)
    cw = mxq(f64(combined_weights).reshape(G, S, E * C), 2, "e4m3")
    return cw @ mxq(expert_outputs.reshape(G, E * C, M), 1, "e4m3")

@@ -1,0 +1,231 @@
+from contextlib import ExitStack
+
+import concourse.mybir as mybir
+from concourse.masks import make_identity
+
+BF16 = mybir.dt.bfloat16
+F32 = mybir.dt.float32
+I32 = mybir.dt.int32
+U32 = mybir.dt.uint32
+U8 = mybir.dt.uint8
+FP8X4 = mybir.dt.float8_e4m3fn_x4
+
+G, S, M, H, E, C = 2, 512, 512, 1024, 16, 64
+P = 128
+PACK = 4
+K_PASS = P * PACK
+H_PASSES = H // K_PASS
+HALVES = E * C // K_PASS
+HALF_EXPERTS = E // HALVES
+PAIRS = E // 2
+M_CHUNK = P
+M_CHUNKS = M // M_CHUNK
+S_TILES = S // P
+BANKS = 8
+H_LOAD = 4
+H_SLOT = 3 * C
+
+VECTOR_GROUPS = 72
+
+FLOPS = 2 * E * G * C * H * M + 2 * G * S * E * C * M
+
+
+def copy_by_turns(nc, piece, out, in_):
+    if piece % 2 == 0:
+        nc.vector.tensor_copy(out=out, in_=in_)
+    else:
+        nc.scalar.copy(out=out, in_=in_)
+
+
+def tile_flaxpositionwisemoelayer_pb_kernel(tc, h, wo, combined_weights, out):
+    nc = tc.nc
+    with ExitStack() as ctx:
+        keep = ctx.enter_context(tc.tile_pool(name="keep", bufs=1))
+        wo_raw_pool = ctx.enter_context(tc.tile_pool(name="wo_raw", bufs=4))
+        wo_grouped_pool = ctx.enter_context(tc.tile_pool(name="wo_grouped", bufs=4))
+        wo_mx_pool = ctx.enter_context(tc.tile_pool(name="wo_mx", bufs=6))
+        grouped_pool = ctx.enter_context(tc.tile_pool(name="grouped", bufs=3))
+        eo_grouped_pool = ctx.enter_context(tc.tile_pool(name="eo_grouped", bufs=2))
+        result_pool = ctx.enter_context(tc.tile_pool(name="result", bufs=4))
+        psum = ctx.enter_context(tc.psum_pool(name="psum", bufs=1))
+
+        def bank(index, shape, dtype):
+            tag = "bank%d" % (index % BANKS)
+            return psum.tile(shape, dtype, name=tag, tag=tag)
+
+        h_raw = []
+        for i in range(E // H_LOAD):
+            h_part = keep.tile([P, H_LOAD * H], BF16, name="h_raw%d" % i)
+            nc.sync.dma_start(
+                out=h_part[:].rearrange("p (e k) -> p e k", e=H_LOAD),
+                in_=h[i * H_LOAD : (i + 1) * H_LOAD].rearrange("e g c k -> (g c) e k"),
+            )
+            h_raw.append(h_part)
+        cw_raw = []
+        for g in range(G):
+            cw_part = keep.tile([P, S_TILES * E * C], BF16, name="cw_raw%d" % g)
+            nc.sync.dma_start(
+                out=cw_part[:],
+                in_=combined_weights[g].rearrange("(i st) e c -> i (st e c)", st=S_TILES),
+            )
+            cw_raw.append(cw_part)
+
+        identity_f32 = keep.tile([P, P], F32, name="identity_f32")
+        make_identity(nc, identity_f32[:])
+        identity_bf16 = keep.tile([P, P], BF16, name="identity_bf16")
+        make_identity(nc, identity_bf16[:])
+
+        h_words = keep.tile([P, PAIRS * G * H_PASSES * H_SLOT], U32, name="h_words", align_bytes=64)
+        h_scales = keep.tile([P, PAIRS * G * H_PASSES * H_SLOT], U8, name="h_scales", align_bytes=64)
+        cw_words = keep.tile([P, G * S_TILES * HALVES * P], U32, name="cw_words", align_bytes=64)
+        cw_scales = keep.tile([P, G * S_TILES * HALVES * P], U8, name="cw_scales", align_bytes=64)
+        eo_words = keep.tile([P, HALVES * G * M], U32, name="eo_words", align_bytes=64)
+        eo_scales = keep.tile([P, HALVES * G * M], U8, name="eo_scales", align_bytes=64)
+
+        nc.vector.memset(
+            h_words[:].bitcast(I32).rearrange("p (slot w) -> p slot w", w=H_SLOT)[:, :, C : 2 * C], 0
+        )
+        nc.vector.memset(
+            h_scales[:].bitcast(I32).rearrange("p (slot w) -> p slot w", w=H_SLOT // 4)[
+                :, :, C // 4 : 2 * C // 4
+            ],
+            0,
+        )
+
+        def h_slot(pair, g, kp):
+            return ((pair * G + g) * H_PASSES + kp) * H_SLOT
+
+        for e in range(E):
+            h_as_words = h_raw[e // H_LOAD][:].bitcast(F32).rearrange(
+                "p (e kp w u) -> p e kp u w", e=H_LOAD, kp=H_PASSES, u=2
+            )
+            flipped = bank(e, [P, H_PASSES, 2, P], F32)
+            for kp in range(H_PASSES):
+                for u in range(2):
+                    nc.tensor.transpose(
+                        flipped[:, kp, u, :], h_as_words[:, e % H_LOAD, kp, u, :], identity_f32[:]
+                    )
+            h_grouped = grouped_pool.tile([P, H_PASSES * P * PACK], BF16, align_bytes=64)
+            nc.scalar.copy(
+                out=h_grouped[:].bitcast(F32).rearrange("p (kp r u) -> p kp r u", kp=H_PASSES, u=2),
+                in_=flipped[:].rearrange("p kp u r -> p kp r u"),
+            )
+            for kp in range(H_PASSES):
+                for g in range(G):
+                    first = h_slot(e // 2, g, kp) + (e % 2) * 2 * C
+                    rows = (kp * P + g * C) * PACK
+                    nc.vector.quantize_mx(
+                        out=h_words[:, first : first + C].bitcast(FP8X4),
+                        scales=h_scales[:, first : first + C],
+                        in_=h_grouped[:, rows : rows + C * PACK],
+                    )
+
+        for g in range(G):
+            for st in range(S_TILES):
+                cw_grouped = grouped_pool.tile([P, HALVES * P * PACK], BF16, align_bytes=64)
+                for half in range(HALVES):
+                    flipped = bank((g * S_TILES + st) * HALVES + half, [P, PACK, P], BF16)
+                    for t in range(PACK):
+                        k2 = st * E * C + half * K_PASS + t * P
+                        nc.tensor.transpose(
+                            flipped[:, t, :], cw_raw[g][:, k2 : k2 + P], identity_bf16[:]
+                        )
+                    copy_by_turns(
+                        nc,
+                        half,
+                        out=cw_grouped[:, half * K_PASS : (half + 1) * K_PASS].rearrange(
+                            "p (i t) -> p i t", t=PACK
+                        ),
+                        in_=flipped[:].rearrange("p t i -> p i t"),
+                    )
+                first = (g * S_TILES + st) * HALVES * P
+                nc.vector.quantize_mx(
+                    out=cw_words[:, first : first + HALVES * P].bitcast(FP8X4),
+                    scales=cw_scales[:, first : first + HALVES * P],
+                    in_=cw_grouped[:],
+                )
+
+        eo_banks = {}
+        for e in range(E):
+            half = e // HALF_EXPERTS
+            t = (e % HALF_EXPERTS) // 2
+            odd = e % 2
+
+            wo_raw = wo_raw_pool.tile([P, H_PASSES * PACK * M], BF16)
+            nc.sync.dma_start(
+                out=wo_raw[:].rearrange("p (kp r) -> p kp r", kp=H_PASSES),
+                in_=wo[e].rearrange("(kp p j) m -> p kp (j m)", kp=H_PASSES, j=PACK),
+            )
+            wo_words = wo_mx_pool.tile([P, H_PASSES * M], U32, align_bytes=64)
+            wo_scales = wo_mx_pool.tile([P, H_PASSES * M], U8, align_bytes=64)
+            for kp in range(H_PASSES):
+                wo_grouped = wo_grouped_pool.tile([P, M * PACK], BF16, align_bytes=64)
+                rows = wo_raw[:, kp * PACK * M : (kp + 1) * PACK * M].rearrange(
+                    "p (j c i) -> p c j i", j=PACK, i=4
+                )
+                columns = wo_grouped[:].rearrange("p (c i j) -> p c j i", i=4, j=PACK)
+                nc.vector.tensor_copy(out=columns[:, :VECTOR_GROUPS], in_=rows[:, :VECTOR_GROUPS])
+                nc.scalar.copy(out=columns[:, VECTOR_GROUPS:], in_=rows[:, VECTOR_GROUPS:])
+                nc.vector.quantize_mx(
+                    out=wo_words[:, kp * M : (kp + 1) * M].bitcast(FP8X4),
+                    scales=wo_scales[:, kp * M : (kp + 1) * M],
+                    in_=wo_grouped[:],
+                )
+
+            if e % HALF_EXPERTS == 0:
+                for g in range(G):
+                    for mc in range(M_CHUNKS):
+                        eo_banks[(g, mc)] = bank(g * M_CHUNKS + mc, [P, PACK, M_CHUNK], F32)
+            for g in range(G):
+                for mc in range(M_CHUNKS):
+                    for kp in range(H_PASSES):
+                        window = h_slot(e // 2, g, kp) + odd * C
+                        cols = kp * M + mc * M_CHUNK
+                        nc.tensor.matmul_mx(
+                            out=eo_banks[(g, mc)][:, t, :],
+                            lhsT=h_words[:, window : window + P].bitcast(FP8X4),
+                            lhsT_scale=h_scales[:, window : window + P],
+                            rhs=wo_words[:, cols : cols + M_CHUNK].bitcast(FP8X4),
+                            rhs_scale=wo_scales[:, cols : cols + M_CHUNK],
+                            start=(odd == 0 and kp == 0),
+                            stop=(odd == 1 and kp == H_PASSES - 1),
+                        )
+
+            if e % HALF_EXPERTS == HALF_EXPERTS - 1:
+                for g in range(G):
+                    eo_grouped = eo_grouped_pool.tile([P, M * PACK], BF16, align_bytes=64)
+                    for mc in range(M_CHUNKS):
+                        copy_by_turns(
+                            nc,
+                            mc,
+                            out=eo_grouped[:, mc * K_PASS : (mc + 1) * K_PASS].rearrange(
+                                "p (m t) -> p m t", t=PACK
+                            ),
+                            in_=eo_banks[(g, mc)][:].rearrange("p t m -> p m t"),
+                        )
+                    first = (half * G + g) * M
+                    nc.vector.quantize_mx(
+                        out=eo_words[:, first : first + M].bitcast(FP8X4),
+                        scales=eo_scales[:, first : first + M],
+                        in_=eo_grouped[:],
+                    )
+
+        out_rows = out.rearrange("g (i st) m -> i g st m", st=S_TILES)
+        for g in range(G):
+            for st in range(S_TILES):
+                acc = bank(g * S_TILES + st, [P, M], F32)
+                for half in range(HALVES):
+                    tokens = ((g * S_TILES + st) * HALVES + half) * P
+                    cols = (half * G + g) * M
+                    nc.tensor.matmul_mx(
+                        out=acc[:],
+                        lhsT=cw_words[:, tokens : tokens + P].bitcast(FP8X4),
+                        lhsT_scale=cw_scales[:, tokens : tokens + P],
+                        rhs=eo_words[:, cols : cols + M].bitcast(FP8X4),
+                        rhs_scale=eo_scales[:, cols : cols + M],
+                        start=(half == 0),
+                        stop=(half == HALVES - 1),
+                    )
+                result = result_pool.tile([P, M], F32)
+                copy_by_turns(nc, st, out=result[:], in_=acc[:])
+                nc.sync.dma_start(out=out_rows[:, g, st, :], in_=result[:])

@@ -22,10 +22,11 @@ M_CHUNK = P
 M_CHUNKS = M // M_CHUNK
 S_TILES = S // P
 BANKS = 8
-H_LOAD = 4
 H_SLOT = 3 * C
+COLUMN_GROUPS = M // 4
 
-VECTOR_GROUPS = 72
+VECTOR_GROUPS_EARLY = 84
+VECTOR_GROUPS_LATE = 72
 
 FLOPS = 2 * E * G * C * H * M + 2 * G * S * E * C * M
 
@@ -41,9 +42,10 @@ def tile_flaxpositionwisemoelayer_pb_kernel(tc, h, wo, combined_weights, out):
     nc = tc.nc
     with ExitStack() as ctx:
         keep = ctx.enter_context(tc.tile_pool(name="keep", bufs=1))
-        wo_raw_pool = ctx.enter_context(tc.tile_pool(name="wo_raw", bufs=4))
+        h_raw_pool = ctx.enter_context(tc.tile_pool(name="h_raw", bufs=3))
+        wo_raw_pool = ctx.enter_context(tc.tile_pool(name="wo_raw", bufs=8))
         wo_grouped_pool = ctx.enter_context(tc.tile_pool(name="wo_grouped", bufs=4))
-        wo_mx_pool = ctx.enter_context(tc.tile_pool(name="wo_mx", bufs=6))
+        wo_mx_pool = ctx.enter_context(tc.tile_pool(name="wo_mx", bufs=HALF_EXPERTS + 2))
         grouped_pool = ctx.enter_context(tc.tile_pool(name="grouped", bufs=3))
         eo_grouped_pool = ctx.enter_context(tc.tile_pool(name="eo_grouped", bufs=2))
         result_pool = ctx.enter_context(tc.tile_pool(name="result", bufs=4))
@@ -52,23 +54,6 @@ def tile_flaxpositionwisemoelayer_pb_kernel(tc, h, wo, combined_weights, out):
         def bank(index, shape, dtype):
             tag = "bank%d" % (index % BANKS)
             return psum.tile(shape, dtype, name=tag, tag=tag)
-
-        h_raw = []
-        for i in range(E // H_LOAD):
-            h_part = keep.tile([P, H_LOAD * H], BF16, name="h_raw%d" % i)
-            nc.sync.dma_start(
-                out=h_part[:].rearrange("p (e k) -> p e k", e=H_LOAD),
-                in_=h[i * H_LOAD : (i + 1) * H_LOAD].rearrange("e g c k -> (g c) e k"),
-            )
-            h_raw.append(h_part)
-        cw_raw = []
-        for g in range(G):
-            cw_part = keep.tile([P, S_TILES * E * C], BF16, name="cw_raw%d" % g)
-            nc.sync.dma_start(
-                out=cw_part[:],
-                in_=combined_weights[g].rearrange("(i st) e c -> i (st e c)", st=S_TILES),
-            )
-            cw_raw.append(cw_part)
 
         identity_f32 = keep.tile([P, P], F32, name="identity_f32")
         make_identity(nc, identity_f32[:])
@@ -95,91 +80,105 @@ def tile_flaxpositionwisemoelayer_pb_kernel(tc, h, wo, combined_weights, out):
         def h_slot(pair, g, kp):
             return ((pair * G + g) * H_PASSES + kp) * H_SLOT
 
-        for e in range(E):
-            h_as_words = h_raw[e // H_LOAD][:].bitcast(F32).rearrange(
-                "p (e kp w u) -> p e kp u w", e=H_LOAD, kp=H_PASSES, u=2
-            )
-            flipped = bank(e, [P, H_PASSES, 2, P], F32)
-            for kp in range(H_PASSES):
-                for u in range(2):
-                    nc.tensor.transpose(
-                        flipped[:, kp, u, :], h_as_words[:, e % H_LOAD, kp, u, :], identity_f32[:]
-                    )
-            h_grouped = grouped_pool.tile([P, H_PASSES * P * PACK], BF16, align_bytes=64)
-            nc.scalar.copy(
-                out=h_grouped[:].bitcast(F32).rearrange("p (kp r u) -> p kp r u", kp=H_PASSES, u=2),
-                in_=flipped[:].rearrange("p kp u r -> p kp r u"),
-            )
-            for kp in range(H_PASSES):
-                for g in range(G):
-                    first = h_slot(e // 2, g, kp) + (e % 2) * 2 * C
-                    rows = (kp * P + g * C) * PACK
-                    nc.vector.quantize_mx(
-                        out=h_words[:, first : first + C].bitcast(FP8X4),
-                        scales=h_scales[:, first : first + C],
-                        in_=h_grouped[:, rows : rows + C * PACK],
-                    )
-
-        for g in range(G):
-            for st in range(S_TILES):
-                cw_grouped = grouped_pool.tile([P, HALVES * P * PACK], BF16, align_bytes=64)
-                for half in range(HALVES):
-                    flipped = bank((g * S_TILES + st) * HALVES + half, [P, PACK, P], BF16)
-                    for t in range(PACK):
-                        k2 = st * E * C + half * K_PASS + t * P
-                        nc.tensor.transpose(
-                            flipped[:, t, :], cw_raw[g][:, k2 : k2 + P], identity_bf16[:]
-                        )
-                    copy_by_turns(
-                        nc,
-                        half,
-                        out=cw_grouped[:, half * K_PASS : (half + 1) * K_PASS].rearrange(
-                            "p (i t) -> p i t", t=PACK
-                        ),
-                        in_=flipped[:].rearrange("p t i -> p i t"),
-                    )
-                first = (g * S_TILES + st) * HALVES * P
-                nc.vector.quantize_mx(
-                    out=cw_words[:, first : first + HALVES * P].bitcast(FP8X4),
-                    scales=cw_scales[:, first : first + HALVES * P],
-                    in_=cw_grouped[:],
-                )
-
-        eo_banks = {}
-        for e in range(E):
-            half = e // HALF_EXPERTS
-            t = (e % HALF_EXPERTS) // 2
-            odd = e % 2
-
-            wo_raw = wo_raw_pool.tile([P, H_PASSES * PACK * M], BF16)
+        def prepare_h(pair):
+            h_raw = h_raw_pool.tile([P, 2 * H], BF16)
             nc.sync.dma_start(
-                out=wo_raw[:].rearrange("p (kp r) -> p kp r", kp=H_PASSES),
-                in_=wo[e].rearrange("(kp p j) m -> p kp (j m)", kp=H_PASSES, j=PACK),
+                out=h_raw[:].rearrange("p (e k) -> p e k", e=2),
+                in_=h[2 * pair : 2 * pair + 2].rearrange("e g c k -> (g c) e k"),
             )
+            h_as_words = h_raw[:].bitcast(F32).rearrange(
+                "p (e kp w u) -> p e kp u w", e=2, kp=H_PASSES, u=2
+            )
+            for odd in range(2):
+                flipped = bank(4 * pair + odd, [P, H_PASSES, 2, P], F32)
+                for kp in range(H_PASSES):
+                    for u in range(2):
+                        nc.tensor.transpose(
+                            flipped[:, kp, u, :], h_as_words[:, odd, kp, u, :], identity_f32[:]
+                        )
+                h_grouped = grouped_pool.tile([P, H_PASSES * P * PACK], BF16, align_bytes=64)
+                nc.scalar.copy(
+                    out=h_grouped[:].bitcast(F32).rearrange(
+                        "p (kp r u) -> p kp r u", kp=H_PASSES, u=2
+                    ),
+                    in_=flipped[:].rearrange("p kp u r -> p kp r u"),
+                )
+                for kp in range(H_PASSES):
+                    for g in range(G):
+                        first = h_slot(pair, g, kp) + odd * 2 * C
+                        rows = (kp * P + g * C) * PACK
+                        nc.vector.quantize_mx(
+                            out=h_words[:, first : first + C].bitcast(FP8X4),
+                            scales=h_scales[:, first : first + C],
+                            in_=h_grouped[:, rows : rows + C * PACK],
+                        )
+
+        cw_raw = {}
+
+        def load_cw(g):
+            cw_raw[g] = keep.tile([P, S_TILES * E * C], BF16, name="cw_raw%d" % g)
+            nc.sync.dma_start(
+                out=cw_raw[g][:],
+                in_=combined_weights[g].rearrange("(i st) e c -> i (st e c)", st=S_TILES),
+            )
+
+        def prepare_cw(g, st):
+            cw_grouped = grouped_pool.tile([P, HALVES * P * PACK], BF16, align_bytes=64)
+            for half in range(HALVES):
+                flipped = bank(4 * (g * S_TILES + st) + 2 + half, [P, PACK, P], BF16)
+                for t in range(PACK):
+                    k2 = st * E * C + half * K_PASS + t * P
+                    nc.tensor.transpose(flipped[:, t, :], cw_raw[g][:, k2 : k2 + P], identity_bf16[:])
+                nc.scalar.copy(
+                    out=cw_grouped[:, half * K_PASS : (half + 1) * K_PASS].rearrange(
+                        "p (i t) -> p i t", t=PACK
+                    ),
+                    in_=flipped[:].rearrange("p t i -> p i t"),
+                )
+            first = (g * S_TILES + st) * HALVES * P
+            nc.vector.quantize_mx(
+                out=cw_words[:, first : first + HALVES * P].bitcast(FP8X4),
+                scales=cw_scales[:, first : first + HALVES * P],
+                in_=cw_grouped[:],
+            )
+
+        wo_mx = {}
+
+        def prepare_wo(e, vector_groups):
             wo_words = wo_mx_pool.tile([P, H_PASSES * M], U32, align_bytes=64)
             wo_scales = wo_mx_pool.tile([P, H_PASSES * M], U8, align_bytes=64)
+            wo_mx[e] = (wo_words, wo_scales)
             for kp in range(H_PASSES):
-                wo_grouped = wo_grouped_pool.tile([P, M * PACK], BF16, align_bytes=64)
-                rows = wo_raw[:, kp * PACK * M : (kp + 1) * PACK * M].rearrange(
-                    "p (j c i) -> p c j i", j=PACK, i=4
+                wo_raw = wo_raw_pool.tile([P, PACK * M], BF16)
+                nc.sync.dma_start(
+                    out=wo_raw[:],
+                    in_=wo[e, kp * K_PASS : (kp + 1) * K_PASS, :].rearrange("(p j) m -> p (j m)", j=PACK),
                 )
+                wo_grouped = wo_grouped_pool.tile([P, M * PACK], BF16, align_bytes=64)
+                rows = wo_raw[:].rearrange("p (j c i) -> p c j i", j=PACK, i=4)
                 columns = wo_grouped[:].rearrange("p (c i j) -> p c j i", i=4, j=PACK)
-                nc.vector.tensor_copy(out=columns[:, :VECTOR_GROUPS], in_=rows[:, :VECTOR_GROUPS])
-                nc.scalar.copy(out=columns[:, VECTOR_GROUPS:], in_=rows[:, VECTOR_GROUPS:])
+                nc.vector.tensor_copy(out=columns[:, :vector_groups], in_=rows[:, :vector_groups])
+                nc.scalar.copy(out=columns[:, vector_groups:], in_=rows[:, vector_groups:])
                 nc.vector.quantize_mx(
                     out=wo_words[:, kp * M : (kp + 1) * M].bitcast(FP8X4),
                     scales=wo_scales[:, kp * M : (kp + 1) * M],
                     in_=wo_grouped[:],
                 )
 
+        eo_banks = {}
+
+        def first_product(e):
+            t = (e % HALF_EXPERTS) // 2
+            odd = e % 2
             if e % HALF_EXPERTS == 0:
                 for g in range(G):
                     for mc in range(M_CHUNKS):
                         eo_banks[(g, mc)] = bank(g * M_CHUNKS + mc, [P, PACK, M_CHUNK], F32)
-            for g in range(G):
-                for mc in range(M_CHUNKS):
-                    for kp in range(H_PASSES):
-                        window = h_slot(e // 2, g, kp) + odd * C
+            wo_words, wo_scales = wo_mx[e]
+            for kp in range(H_PASSES):
+                for g in range(G):
+                    window = h_slot(e // 2, g, kp) + odd * C
+                    for mc in range(M_CHUNKS):
                         cols = kp * M + mc * M_CHUNK
                         nc.tensor.matmul_mx(
                             out=eo_banks[(g, mc)][:, t, :],
@@ -191,34 +190,50 @@ def tile_flaxpositionwisemoelayer_pb_kernel(tc, h, wo, combined_weights, out):
                             stop=(odd == 1 and kp == H_PASSES - 1),
                         )
 
-            if e % HALF_EXPERTS == HALF_EXPERTS - 1:
-                for g in range(G):
-                    eo_grouped = eo_grouped_pool.tile([P, M * PACK], BF16, align_bytes=64)
-                    for mc in range(M_CHUNKS):
-                        copy_by_turns(
-                            nc,
-                            mc,
-                            out=eo_grouped[:, mc * K_PASS : (mc + 1) * K_PASS].rearrange(
-                                "p (m t) -> p m t", t=PACK
-                            ),
-                            in_=eo_banks[(g, mc)][:].rearrange("p t m -> p m t"),
-                        )
-                    first = (half * G + g) * M
-                    nc.vector.quantize_mx(
-                        out=eo_words[:, first : first + M].bitcast(FP8X4),
-                        scales=eo_scales[:, first : first + M],
-                        in_=eo_grouped[:],
-                    )
+        def quantise_eo(half, g, both_engines):
+            eo_grouped = eo_grouped_pool.tile([P, M * PACK], BF16, align_bytes=64)
+            for mc in range(M_CHUNKS):
+                copy_by_turns(
+                    nc,
+                    mc if both_engines else 1,
+                    out=eo_grouped[:, mc * K_PASS : (mc + 1) * K_PASS].rearrange(
+                        "p (m t) -> p m t", t=PACK
+                    ),
+                    in_=eo_banks[(g, mc)][:].rearrange("p t m -> p m t"),
+                )
+            first = (half * G + g) * M
+            nc.vector.quantize_mx(
+                out=eo_words[:, first : first + M].bitcast(FP8X4),
+                scales=eo_scales[:, first : first + M],
+                in_=eo_grouped[:],
+            )
+
+        for r in range(HALF_EXPERTS):
+            prepare_h(r)
+            prepare_wo(r, VECTOR_GROUPS_EARLY)
+            if r % S_TILES == 0:
+                load_cw(r // S_TILES)
+            prepare_cw(r // S_TILES, r % S_TILES)
+        for e in range(HALF_EXPERTS):
+            first_product(e)
+        for g in range(G):
+            quantise_eo(0, g, False)
+
+        for e in range(HALF_EXPERTS, E):
+            prepare_wo(e, VECTOR_GROUPS_LATE)
+            first_product(e)
+        for g in range(G):
+            quantise_eo(1, g, True)
 
         out_rows = out.rearrange("g (i st) m -> i g st m", st=S_TILES)
         for g in range(G):
-            for st in range(S_TILES):
-                acc = bank(g * S_TILES + st, [P, M], F32)
-                for half in range(HALVES):
+            accs = [bank(g * S_TILES + st, [P, M], F32) for st in range(S_TILES)]
+            for half in range(HALVES):
+                for st in range(S_TILES):
                     tokens = ((g * S_TILES + st) * HALVES + half) * P
                     cols = (half * G + g) * M
                     nc.tensor.matmul_mx(
-                        out=acc[:],
+                        out=accs[st][:],
                         lhsT=cw_words[:, tokens : tokens + P].bitcast(FP8X4),
                         lhsT_scale=cw_scales[:, tokens : tokens + P],
                         rhs=eo_words[:, cols : cols + M].bitcast(FP8X4),
@@ -226,6 +241,7 @@ def tile_flaxpositionwisemoelayer_pb_kernel(tc, h, wo, combined_weights, out):
                         start=(half == 0),
                         stop=(half == HALVES - 1),
                     )
+            for st in range(S_TILES):
                 result = result_pool.tile([P, M], F32)
-                copy_by_turns(nc, st, out=result[:], in_=acc[:])
+                copy_by_turns(nc, st, out=result[:], in_=accs[st][:])
                 nc.sync.dma_start(out=out_rows[:, g, st, :], in_=result[:])

@@ -28,6 +28,11 @@ COLUMN_GROUPS = M // 4
 VECTOR_GROUPS_EARLY = 84
 VECTOR_GROUPS_LATE = 72
 
+SPLIT_EXPERTS = 4
+COLUMN_HALVES = 2
+HALF_M = M // COLUMN_HALVES
+HALF_CHUNKS = M_CHUNKS // COLUMN_HALVES
+
 FLOPS = 2 * E * G * C * H * M + 2 * G * S * E * C * M
 
 
@@ -46,6 +51,7 @@ def tile_flaxpositionwisemoelayer_pb_kernel(tc, h, wo, combined_weights, out):
         wo_raw_pool = ctx.enter_context(tc.tile_pool(name="wo_raw", bufs=8))
         wo_grouped_pool = ctx.enter_context(tc.tile_pool(name="wo_grouped", bufs=4))
         wo_mx_pool = ctx.enter_context(tc.tile_pool(name="wo_mx", bufs=HALF_EXPERTS + 2))
+        wo_mx_cols_pool = ctx.enter_context(tc.tile_pool(name="wo_mx_cols", bufs=4))
         grouped_pool = ctx.enter_context(tc.tile_pool(name="grouped", bufs=3))
         eo_grouped_pool = ctx.enter_context(tc.tile_pool(name="eo_grouped", bufs=2))
         result_pool = ctx.enter_context(tc.tile_pool(name="result", bufs=4))
@@ -165,7 +171,53 @@ def tile_flaxpositionwisemoelayer_pb_kernel(tc, h, wo, combined_weights, out):
                     in_=wo_grouped[:],
                 )
 
+        wo_kept = {}
+
+        def load_wo(e):
+            for kp in range(H_PASSES):
+                wo_raw = wo_raw_pool.tile([P, PACK * M], BF16)
+                nc.sync.dma_start(
+                    out=wo_raw[:],
+                    in_=wo[e, kp * K_PASS : (kp + 1) * K_PASS, :].rearrange("(p j) m -> p (j m)", j=PACK),
+                )
+                wo_kept[(e, kp)] = wo_raw
+
+        def prepare_wo_columns(e, ch):
+            wo_words = wo_mx_cols_pool.tile([P, H_PASSES * HALF_M], U32, align_bytes=64)
+            wo_scales = wo_mx_cols_pool.tile([P, H_PASSES * HALF_M], U8, align_bytes=64)
+            wo_mx[(e, ch)] = (wo_words, wo_scales)
+            wo_grouped = wo_grouped_pool.tile([P, M * PACK], BF16, align_bytes=64)
+            groups = HALF_M // 4
+            for kp in range(H_PASSES):
+                rows = wo_kept[(e, kp)][:].rearrange("p (j c i) -> p c j i", j=PACK, i=4)
+                columns = wo_grouped[:, kp * HALF_M * PACK : (kp + 1) * HALF_M * PACK].rearrange(
+                    "p (c i j) -> p c j i", i=4, j=PACK
+                )
+                copy_by_turns(nc, kp, out=columns, in_=rows[:, ch * groups : (ch + 1) * groups])
+            nc.vector.quantize_mx(
+                out=wo_words[:].bitcast(FP8X4), scales=wo_scales[:], in_=wo_grouped[:]
+            )
+
         eo_banks = {}
+
+        def first_product_columns(e, ch):
+            t = (e % HALF_EXPERTS) // 2
+            odd = e % 2
+            wo_words, wo_scales = wo_mx[(e, ch)]
+            for kp in range(H_PASSES):
+                for g in range(G):
+                    window = h_slot(e // 2, g, kp) + odd * C
+                    for c2 in range(HALF_CHUNKS):
+                        cols = kp * HALF_M + c2 * M_CHUNK
+                        nc.tensor.matmul_mx(
+                            out=eo_banks[(g, ch * HALF_CHUNKS + c2)][:, t, :],
+                            lhsT=h_words[:, window : window + P].bitcast(FP8X4),
+                            lhsT_scale=h_scales[:, window : window + P],
+                            rhs=wo_words[:, cols : cols + M_CHUNK].bitcast(FP8X4),
+                            rhs_scale=wo_scales[:, cols : cols + M_CHUNK],
+                            start=(odd == 0 and kp == 0),
+                            stop=(odd == 1 and kp == H_PASSES - 1),
+                        )
 
         def first_product(e):
             t = (e % HALF_EXPERTS) // 2
@@ -219,29 +271,53 @@ def tile_flaxpositionwisemoelayer_pb_kernel(tc, h, wo, combined_weights, out):
         for g in range(G):
             quantise_eo(0, g, False)
 
-        for e in range(HALF_EXPERTS, E):
+        for e in range(HALF_EXPERTS, E - SPLIT_EXPERTS):
             prepare_wo(e, VECTOR_GROUPS_LATE)
             first_product(e)
-        for g in range(G):
-            quantise_eo(1, g, True)
+        for e in range(E - SPLIT_EXPERTS, E):
+            load_wo(e)
 
         out_rows = out.rearrange("g (i st) m -> i g st m", st=S_TILES)
-        for g in range(G):
-            accs = [bank(g * S_TILES + st, [P, M], F32) for st in range(S_TILES)]
-            for half in range(HALVES):
-                for st in range(S_TILES):
-                    tokens = ((g * S_TILES + st) * HALVES + half) * P
-                    cols = (half * G + g) * M
-                    nc.tensor.matmul_mx(
-                        out=accs[st][:],
-                        lhsT=cw_words[:, tokens : tokens + P].bitcast(FP8X4),
-                        lhsT_scale=cw_scales[:, tokens : tokens + P],
-                        rhs=eo_words[:, cols : cols + M].bitcast(FP8X4),
-                        rhs_scale=eo_scales[:, cols : cols + M],
-                        start=(half == 0),
-                        stop=(half == HALVES - 1),
+        for ch in range(COLUMN_HALVES):
+            for e in range(E - SPLIT_EXPERTS, E):
+                prepare_wo_columns(e, ch)
+                first_product_columns(e, ch)
+            for g in range(G):
+                eo_grouped = eo_grouped_pool.tile([P, M * PACK], BF16, align_bytes=64)
+                for c2 in range(HALF_CHUNKS):
+                    copy_by_turns(
+                        nc,
+                        c2,
+                        out=eo_grouped[:, c2 * K_PASS : (c2 + 1) * K_PASS].rearrange(
+                            "p (m t) -> p m t", t=PACK
+                        ),
+                        in_=eo_banks[(g, ch * HALF_CHUNKS + c2)][:].rearrange("p t m -> p m t"),
                     )
-            for st in range(S_TILES):
-                result = result_pool.tile([P, M], F32)
-                copy_by_turns(nc, st, out=result[:], in_=accs[st][:])
-                nc.sync.dma_start(out=out_rows[:, g, st, :], in_=result[:])
+                first = (G + g) * M + ch * HALF_M
+                nc.vector.quantize_mx(
+                    out=eo_words[:, first : first + HALF_M].bitcast(FP8X4),
+                    scales=eo_scales[:, first : first + HALF_M],
+                    in_=eo_grouped[:, : HALF_M * PACK],
+                )
+            for g in range(G):
+                for q in range(S_TILES // 2):
+                    acc = bank(g * M_CHUNKS + ch * HALF_CHUNKS + q, [P, 2, HALF_M], F32)
+                    for s2 in range(2):
+                        st = 2 * q + s2
+                        for half in range(HALVES):
+                            tokens = ((g * S_TILES + st) * HALVES + half) * P
+                            cols = (half * G + g) * M + ch * HALF_M
+                            nc.tensor.matmul_mx(
+                                out=acc[:, s2, :],
+                                lhsT=cw_words[:, tokens : tokens + P].bitcast(FP8X4),
+                                lhsT_scale=cw_scales[:, tokens : tokens + P],
+                                rhs=eo_words[:, cols : cols + HALF_M].bitcast(FP8X4),
+                                rhs_scale=eo_scales[:, cols : cols + HALF_M],
+                                start=(half == 0),
+                                stop=(half == HALVES - 1),
+                            )
+                    result = result_pool.tile([P, 2, HALF_M], F32)
+                    copy_by_turns(nc, q, out=result[:], in_=acc[:])
+                    nc.sync.dma_start(
+                        out=out_rows[:, g, 2 * q : 2 * q + 2, ch * HALF_M : (ch + 1) * HALF_M], in_=result[:]
+                    )

@@ -23,6 +23,7 @@ M_CHUNKS = M // M_CHUNK
 S_TILES = S // P
 BANKS = 8
 H_SLOT = 3 * C
+H_SLOTS = PAIRS * G * H_PASSES
 COLUMN_GROUPS = M // 4
 
 VECTOR_GROUPS_EARLY = 84
@@ -66,19 +67,19 @@ def tile_flaxpositionwisemoelayer_pb_kernel(tc, h, wo, combined_weights, out):
         identity_bf16 = keep.tile([P, P], BF16, name="identity_bf16")
         make_identity(nc, identity_bf16[:])
 
-        h_words = keep.tile([P, PAIRS * G * H_PASSES * H_SLOT], U32, name="h_words", align_bytes=64)
-        h_scales = keep.tile([P, PAIRS * G * H_PASSES * H_SLOT], U8, name="h_scales", align_bytes=64)
+        h_words = keep.tile([P, (H_SLOTS + 1) * H_SLOT], U32, name="h_words", align_bytes=64)
+        h_scales = keep.tile([P, (H_SLOTS + 1) * H_SLOT], U8, name="h_scales", align_bytes=64)
         cw_words = keep.tile([P, G * S_TILES * HALVES * P], U32, name="cw_words", align_bytes=64)
         cw_scales = keep.tile([P, G * S_TILES * HALVES * P], U8, name="cw_scales", align_bytes=64)
         eo_words = keep.tile([P, HALVES * G * M], U32, name="eo_words", align_bytes=64)
         eo_scales = keep.tile([P, HALVES * G * M], U8, name="eo_scales", align_bytes=64)
 
         nc.vector.memset(
-            h_words[:].bitcast(I32).rearrange("p (slot w) -> p slot w", w=H_SLOT)[:, :, C : 2 * C], 0
+            h_words[:].bitcast(I32).rearrange("p (slot w) -> p slot w", w=H_SLOT)[:, :, :C], 0
         )
         nc.vector.memset(
             h_scales[:].bitcast(I32).rearrange("p (slot w) -> p slot w", w=H_SLOT // 4)[
-                :, :, C // 4 : 2 * C // 4
+                :, :, : C // 4
             ],
             0,
         )
@@ -95,6 +96,10 @@ def tile_flaxpositionwisemoelayer_pb_kernel(tc, h, wo, combined_weights, out):
             h_as_words = h_raw[:].bitcast(F32).rearrange(
                 "p (e kp w u) -> p e kp u w", e=2, kp=H_PASSES, u=2
             )
+            h_grouped = grouped_pool.tile([P, H_PASSES * G * 2 * C * PACK], BF16, align_bytes=64)
+            h_grouped_words = h_grouped[:].bitcast(F32).rearrange(
+                "p (kp g o c u) -> p kp g o c u", kp=H_PASSES, g=G, o=2, u=2
+            )
             for odd in range(2):
                 flipped = bank(4 * pair + odd, [P, H_PASSES, 2, P], F32)
                 for kp in range(H_PASSES):
@@ -102,22 +107,19 @@ def tile_flaxpositionwisemoelayer_pb_kernel(tc, h, wo, combined_weights, out):
                         nc.tensor.transpose(
                             flipped[:, kp, u, :], h_as_words[:, odd, kp, u, :], identity_f32[:]
                         )
-                h_grouped = grouped_pool.tile([P, H_PASSES * P * PACK], BF16, align_bytes=64)
                 nc.scalar.copy(
-                    out=h_grouped[:].bitcast(F32).rearrange(
-                        "p (kp r u) -> p kp r u", kp=H_PASSES, u=2
-                    ),
-                    in_=flipped[:].rearrange("p kp u r -> p kp r u"),
+                    out=h_grouped_words[:, :, :, 1 - odd, :, :],
+                    in_=flipped[:].rearrange("p kp u (g c) -> p kp g c u", g=G),
                 )
-                for kp in range(H_PASSES):
-                    for g in range(G):
-                        first = h_slot(pair, g, kp) + odd * 2 * C
-                        rows = (kp * P + g * C) * PACK
-                        nc.vector.quantize_mx(
-                            out=h_words[:, first : first + C].bitcast(FP8X4),
-                            scales=h_scales[:, first : first + C],
-                            in_=h_grouped[:, rows : rows + C * PACK],
-                        )
+            for kp in range(H_PASSES):
+                for g in range(G):
+                    first = h_slot(pair, g, kp) + C
+                    rows = (kp * G + g) * 2 * C * PACK
+                    nc.vector.quantize_mx(
+                        out=h_words[:, first : first + 2 * C].bitcast(FP8X4),
+                        scales=h_scales[:, first : first + 2 * C],
+                        in_=h_grouped[:, rows : rows + 2 * C * PACK],
+                    )
 
         cw_raw = {}
 
@@ -206,7 +208,7 @@ def tile_flaxpositionwisemoelayer_pb_kernel(tc, h, wo, combined_weights, out):
             wo_words, wo_scales = wo_mx[(e, ch)]
             for kp in range(H_PASSES):
                 for g in range(G):
-                    window = h_slot(e // 2, g, kp) + odd * C
+                    window = h_slot(e // 2, g, kp) + (1 - odd) * 2 * C
                     for c2 in range(HALF_CHUNKS):
                         cols = kp * HALF_M + c2 * M_CHUNK
                         nc.tensor.matmul_mx(
@@ -229,7 +231,7 @@ def tile_flaxpositionwisemoelayer_pb_kernel(tc, h, wo, combined_weights, out):
             wo_words, wo_scales = wo_mx[e]
             for kp in range(H_PASSES):
                 for g in range(G):
-                    window = h_slot(e // 2, g, kp) + odd * C
+                    window = h_slot(e // 2, g, kp) + (1 - odd) * 2 * C
                     for mc in range(M_CHUNKS):
                         cols = kp * M + mc * M_CHUNK
                         nc.tensor.matmul_mx(

@@ -26,8 +26,8 @@ H_SLOT = 3 * C
 H_SLOTS = PAIRS * G * H_PASSES
 COLUMN_GROUPS = M // 4
 
-VECTOR_GROUPS_EARLY = 84
-VECTOR_GROUPS_LATE = 72
+VECTOR_GROUPS_EARLY = 40
+VECTOR_GROUPS_LATE = 16
 
 SPLIT_EXPERTS = 4
 COLUMN_HALVES = 2
@@ -50,7 +50,7 @@ def tile_flaxpositionwisemoelayer_pb_kernel(tc, h, wo, combined_weights, out):
         keep = ctx.enter_context(tc.tile_pool(name="keep", bufs=1))
         h_raw_pool = ctx.enter_context(tc.tile_pool(name="h_raw", bufs=3))
         wo_raw_pool = ctx.enter_context(tc.tile_pool(name="wo_raw", bufs=8))
-        wo_grouped_pool = ctx.enter_context(tc.tile_pool(name="wo_grouped", bufs=4))
+        wo_grouped_pool = ctx.enter_context(tc.tile_pool(name="wo_grouped", bufs=3))
         wo_mx_pool = ctx.enter_context(tc.tile_pool(name="wo_mx", bufs=HALF_EXPERTS + 2))
         wo_mx_cols_pool = ctx.enter_context(tc.tile_pool(name="wo_mx_cols", bufs=4))
         grouped_pool = ctx.enter_context(tc.tile_pool(name="grouped", bufs=3))
@@ -156,22 +156,23 @@ def tile_flaxpositionwisemoelayer_pb_kernel(tc, h, wo, combined_weights, out):
             wo_words = wo_mx_pool.tile([P, H_PASSES * M], U32, align_bytes=64)
             wo_scales = wo_mx_pool.tile([P, H_PASSES * M], U8, align_bytes=64)
             wo_mx[e] = (wo_words, wo_scales)
+            wo_grouped = wo_grouped_pool.tile([P, H_PASSES * M * PACK], BF16, align_bytes=64)
             for kp in range(H_PASSES):
                 wo_raw = wo_raw_pool.tile([P, PACK * M], BF16)
                 nc.sync.dma_start(
                     out=wo_raw[:],
                     in_=wo[e, kp * K_PASS : (kp + 1) * K_PASS, :].rearrange("(p j) m -> p (j m)", j=PACK),
                 )
-                wo_grouped = wo_grouped_pool.tile([P, M * PACK], BF16, align_bytes=64)
                 rows = wo_raw[:].rearrange("p (j c i) -> p c j i", j=PACK, i=4)
-                columns = wo_grouped[:].rearrange("p (c i j) -> p c j i", i=4, j=PACK)
-                nc.vector.tensor_copy(out=columns[:, :vector_groups], in_=rows[:, :vector_groups])
-                nc.scalar.copy(out=columns[:, vector_groups:], in_=rows[:, vector_groups:])
-                nc.vector.quantize_mx(
-                    out=wo_words[:, kp * M : (kp + 1) * M].bitcast(FP8X4),
-                    scales=wo_scales[:, kp * M : (kp + 1) * M],
-                    in_=wo_grouped[:],
+                columns = wo_grouped[:, kp * M * PACK : (kp + 1) * M * PACK].rearrange(
+                    "p (c i j) -> p c j i", i=4, j=PACK
                 )
+                if kp == 0:
+                    nc.vector.tensor_copy(out=columns, in_=rows)
+                else:
+                    nc.vector.tensor_copy(out=columns[:, :vector_groups], in_=rows[:, :vector_groups])
+                    nc.scalar.copy(out=columns[:, vector_groups:], in_=rows[:, vector_groups:])
+            nc.vector.quantize_mx(out=wo_words[:].bitcast(FP8X4), scales=wo_scales[:], in_=wo_grouped[:])
 
         wo_kept = {}
 
@@ -188,7 +189,7 @@ def tile_flaxpositionwisemoelayer_pb_kernel(tc, h, wo, combined_weights, out):
             wo_words = wo_mx_cols_pool.tile([P, H_PASSES * HALF_M], U32, align_bytes=64)
             wo_scales = wo_mx_cols_pool.tile([P, H_PASSES * HALF_M], U8, align_bytes=64)
             wo_mx[(e, ch)] = (wo_words, wo_scales)
-            wo_grouped = wo_grouped_pool.tile([P, M * PACK], BF16, align_bytes=64)
+            wo_grouped = wo_grouped_pool.tile([P, H_PASSES * HALF_M * PACK], BF16, align_bytes=64)
             groups = HALF_M // 4
             for kp in range(H_PASSES):
                 rows = wo_kept[(e, kp)][:].rearrange("p (j c i) -> p c j i", j=PACK, i=4)

@@ -54,6 +54,7 @@ def tile_flaxpositionwisemoelayer_pb_kernel(tc, h, wo, combined_weights, out):
         wo_mx_pool = ctx.enter_context(tc.tile_pool(name="wo_mx", bufs=HALF_EXPERTS + 2))
         wo_mx_cols_pool = ctx.enter_context(tc.tile_pool(name="wo_mx_cols", bufs=4))
         grouped_pool = ctx.enter_context(tc.tile_pool(name="grouped", bufs=3))
+        cw_grouped_pool = ctx.enter_context(tc.tile_pool(name="cw_grouped", bufs=2))
         eo_grouped_pool = ctx.enter_context(tc.tile_pool(name="eo_grouped", bufs=2))
         result_pool = ctx.enter_context(tc.tile_pool(name="result", bufs=4))
         psum = ctx.enter_context(tc.psum_pool(name="psum", bufs=1))
@@ -61,6 +62,12 @@ def tile_flaxpositionwisemoelayer_pb_kernel(tc, h, wo, combined_weights, out):
         def bank(index, shape, dtype):
             tag = "bank%d" % (index % BANKS)
             return psum.tile(shape, dtype, name=tag, tag=tag)
+
+        banks_taken = []
+
+        def next_bank(shape, dtype):
+            banks_taken.append(1)
+            return bank(len(banks_taken) - 1, shape, dtype)
 
         identity_f32 = keep.tile([P, P], F32, name="identity_f32")
         make_identity(nc, identity_f32[:])
@@ -101,7 +108,7 @@ def tile_flaxpositionwisemoelayer_pb_kernel(tc, h, wo, combined_weights, out):
                 "p (kp g o c u) -> p kp g o c u", kp=H_PASSES, g=G, o=2, u=2
             )
             for odd in range(2):
-                flipped = bank(4 * pair + odd, [P, H_PASSES, 2, P], F32)
+                flipped = next_bank([P, H_PASSES, 2, P], F32)
                 for kp in range(H_PASSES):
                     for u in range(2):
                         nc.tensor.transpose(
@@ -130,33 +137,41 @@ def tile_flaxpositionwisemoelayer_pb_kernel(tc, h, wo, combined_weights, out):
                 in_=combined_weights[g].rearrange("(i st) e c -> i (st e c)", st=S_TILES),
             )
 
+        cw_grouped_now = {}
+
         def prepare_cw(g, st):
-            cw_grouped = grouped_pool.tile([P, HALVES * P * PACK], BF16, align_bytes=64)
+            if st % 2 == 0:
+                cw_grouped = cw_grouped_pool.tile([P, 2 * HALVES * P * PACK], BF16, align_bytes=64)
+                cw_grouped_now[g] = cw_grouped
+            flipped = next_bank([P, HALVES, PACK, P], BF16)
             for half in range(HALVES):
-                flipped = bank(4 * (g * S_TILES + st) + 2 + half, [P, PACK, P], BF16)
                 for t in range(PACK):
                     k2 = st * E * C + half * K_PASS + t * P
-                    nc.tensor.transpose(flipped[:, t, :], cw_raw[g][:, k2 : k2 + P], identity_bf16[:])
-                nc.scalar.copy(
-                    out=cw_grouped[:, half * K_PASS : (half + 1) * K_PASS].rearrange(
-                        "p (i t) -> p i t", t=PACK
-                    ),
-                    in_=flipped[:].rearrange("p t i -> p i t"),
-                )
-            first = (g * S_TILES + st) * HALVES * P
-            nc.vector.quantize_mx(
-                out=cw_words[:, first : first + HALVES * P].bitcast(FP8X4),
-                scales=cw_scales[:, first : first + HALVES * P],
-                in_=cw_grouped[:],
+                    nc.tensor.transpose(
+                        flipped[:, half, t, :], cw_raw[g][:, k2 : k2 + P], identity_bf16[:]
+                    )
+            values = (st % 2) * HALVES * K_PASS
+            nc.scalar.copy(
+                out=cw_grouped_now[g][:, values : values + HALVES * K_PASS].rearrange(
+                    "p (half i t) -> p half i t", half=HALVES, t=PACK
+                ),
+                in_=flipped[:].rearrange("p half t i -> p half i t"),
             )
+            if st % 2 == 1:
+                first = (g * S_TILES + st - 1) * HALVES * P
+                nc.vector.quantize_mx(
+                    out=cw_words[:, first : first + 2 * HALVES * P].bitcast(FP8X4),
+                    scales=cw_scales[:, first : first + 2 * HALVES * P],
+                    in_=cw_grouped_now[g][:],
+                )
 
         wo_mx = {}
 
-        def prepare_wo(e, vector_groups):
-            wo_words = wo_mx_pool.tile([P, H_PASSES * M], U32, align_bytes=64)
-            wo_scales = wo_mx_pool.tile([P, H_PASSES * M], U8, align_bytes=64)
-            wo_mx[e] = (wo_words, wo_scales)
+        wo_grouped_kept = {}
+
+        def regroup_wo(e, vector_groups):
             wo_grouped = wo_grouped_pool.tile([P, H_PASSES * M * PACK], BF16, align_bytes=64)
+            wo_grouped_kept[e] = wo_grouped
             for kp in range(H_PASSES):
                 wo_raw = wo_raw_pool.tile([P, PACK * M], BF16)
                 nc.sync.dma_start(
@@ -172,7 +187,14 @@ def tile_flaxpositionwisemoelayer_pb_kernel(tc, h, wo, combined_weights, out):
                 else:
                     nc.vector.tensor_copy(out=columns[:, :vector_groups], in_=rows[:, :vector_groups])
                     nc.scalar.copy(out=columns[:, vector_groups:], in_=rows[:, vector_groups:])
-            nc.vector.quantize_mx(out=wo_words[:].bitcast(FP8X4), scales=wo_scales[:], in_=wo_grouped[:])
+
+        def quantise_wo(e):
+            wo_words = wo_mx_pool.tile([P, H_PASSES * M], U32, align_bytes=64)
+            wo_scales = wo_mx_pool.tile([P, H_PASSES * M], U8, align_bytes=64)
+            wo_mx[e] = (wo_words, wo_scales)
+            nc.vector.quantize_mx(
+                out=wo_words[:].bitcast(FP8X4), scales=wo_scales[:], in_=wo_grouped_kept[e][:]
+            )
 
         wo_kept = {}
 
@@ -185,11 +207,9 @@ def tile_flaxpositionwisemoelayer_pb_kernel(tc, h, wo, combined_weights, out):
                 )
                 wo_kept[(e, kp)] = wo_raw
 
-        def prepare_wo_columns(e, ch):
-            wo_words = wo_mx_cols_pool.tile([P, H_PASSES * HALF_M], U32, align_bytes=64)
-            wo_scales = wo_mx_cols_pool.tile([P, H_PASSES * HALF_M], U8, align_bytes=64)
-            wo_mx[(e, ch)] = (wo_words, wo_scales)
+        def regroup_wo_columns(e, ch):
             wo_grouped = wo_grouped_pool.tile([P, H_PASSES * HALF_M * PACK], BF16, align_bytes=64)
+            wo_grouped_kept[(e, ch)] = wo_grouped
             groups = HALF_M // 4
             for kp in range(H_PASSES):
                 rows = wo_kept[(e, kp)][:].rearrange("p (j c i) -> p c j i", j=PACK, i=4)
@@ -197,8 +217,13 @@ def tile_flaxpositionwisemoelayer_pb_kernel(tc, h, wo, combined_weights, out):
                     "p (c i j) -> p c j i", i=4, j=PACK
                 )
                 copy_by_turns(nc, kp, out=columns, in_=rows[:, ch * groups : (ch + 1) * groups])
+
+        def quantise_wo_columns(e, ch):
+            wo_words = wo_mx_cols_pool.tile([P, H_PASSES * HALF_M], U32, align_bytes=64)
+            wo_scales = wo_mx_cols_pool.tile([P, H_PASSES * HALF_M], U8, align_bytes=64)
+            wo_mx[(e, ch)] = (wo_words, wo_scales)
             nc.vector.quantize_mx(
-                out=wo_words[:].bitcast(FP8X4), scales=wo_scales[:], in_=wo_grouped[:]
+                out=wo_words[:].bitcast(FP8X4), scales=wo_scales[:], in_=wo_grouped_kept[(e, ch)][:]
             )
 
         eo_banks = {}
@@ -265,26 +290,28 @@ def tile_flaxpositionwisemoelayer_pb_kernel(tc, h, wo, combined_weights, out):
 
         for r in range(HALF_EXPERTS):
             prepare_h(r)
-            prepare_wo(r, VECTOR_GROUPS_EARLY)
+            regroup_wo(r, VECTOR_GROUPS_EARLY)
+            if r > 0:
+                quantise_wo(r - 1)
             if r % S_TILES == 0:
                 load_cw(r // S_TILES)
             prepare_cw(r // S_TILES, r % S_TILES)
+        regroup_wo(HALF_EXPERTS, VECTOR_GROUPS_LATE)
+        quantise_wo(HALF_EXPERTS - 1)
         for e in range(HALF_EXPERTS):
             first_product(e)
         for g in range(G):
             quantise_eo(0, g, False)
 
-        for e in range(HALF_EXPERTS, E - SPLIT_EXPERTS):
-            prepare_wo(e, VECTOR_GROUPS_LATE)
-            first_product(e)
+        for e in range(HALF_EXPERTS + 1, E - SPLIT_EXPERTS):
+            regroup_wo(e, VECTOR_GROUPS_LATE)
+            quantise_wo(e - 1)
+            first_product(e - 1)
         for e in range(E - SPLIT_EXPERTS, E):
             load_wo(e)
 
         out_rows = out.rearrange("g (i st) m -> i g st m", st=S_TILES)
-        for ch in range(COLUMN_HALVES):
-            for e in range(E - SPLIT_EXPERTS, E):
-                prepare_wo_columns(e, ch)
-                first_product_columns(e, ch)
+        def finish_columns(ch):
             for g in range(G):
                 eo_grouped = eo_grouped_pool.tile([P, M * PACK], BF16, align_bytes=64)
                 for c2 in range(HALF_CHUNKS):
@@ -324,3 +351,15 @@ def tile_flaxpositionwisemoelayer_pb_kernel(tc, h, wo, combined_weights, out):
                     nc.sync.dma_start(
                         out=out_rows[:, g, 2 * q : 2 * q + 2, ch * HALF_M : (ch + 1) * HALF_M], in_=result[:]
                     )
+
+        regroup_wo_columns(E - SPLIT_EXPERTS, 0)
+        quantise_wo(E - SPLIT_EXPERTS - 1)
+        first_product(E - SPLIT_EXPERTS - 1)
+        pieces = [(e, ch) for ch in range(COLUMN_HALVES) for e in range(E - SPLIT_EXPERTS, E)]
+        for i in range(len(pieces)):
+            if i + 1 < len(pieces):
+                regroup_wo_columns(pieces[i + 1][0], pieces[i + 1][1])
+            quantise_wo_columns(pieces[i][0], pieces[i][1])
+            first_product_columns(pieces[i][0], pieces[i][1])
+            if pieces[i][0] == E - 1:
+                finish_columns(pieces[i][1])

@@ -94,30 +94,45 @@ def tile_flaxpositionwisemoelayer_pb_kernel(tc, h, wo, combined_weights, out):
         def h_slot(pair, g, kp):
             return ((pair * G + g) * H_PASSES + kp) * H_SLOT
 
-        def prepare_h(pair):
+        h_kept = {}
+        h_flipped = {}
+        h_grouped_kept = {}
+
+        def load_h(pair):
             h_raw = h_raw_pool.tile([P, 2 * H], BF16)
             nc.sync.dma_start(
                 out=h_raw[:].rearrange("p (e k) -> p e k", e=2),
                 in_=h[2 * pair : 2 * pair + 2].rearrange("e g c k -> (g c) e k"),
             )
-            h_as_words = h_raw[:].bitcast(F32).rearrange(
+            h_kept[pair] = h_raw
+
+        def transpose_h(pair):
+            h_as_words = h_kept[pair][:].bitcast(F32).rearrange(
                 "p (e kp w u) -> p e kp u w", e=2, kp=H_PASSES, u=2
-            )
-            h_grouped = grouped_pool.tile([P, H_PASSES * G * 2 * C * PACK], BF16, align_bytes=64)
-            h_grouped_words = h_grouped[:].bitcast(F32).rearrange(
-                "p (kp g o c u) -> p kp g o c u", kp=H_PASSES, g=G, o=2, u=2
             )
             for odd in range(2):
                 flipped = next_bank([P, H_PASSES, 2, P], F32)
+                h_flipped[(pair, odd)] = flipped
                 for kp in range(H_PASSES):
                     for u in range(2):
                         nc.tensor.transpose(
                             flipped[:, kp, u, :], h_as_words[:, odd, kp, u, :], identity_f32[:]
                         )
+
+        def copy_h(pair):
+            h_grouped = grouped_pool.tile([P, H_PASSES * G * 2 * C * PACK], BF16, align_bytes=64)
+            h_grouped_kept[pair] = h_grouped
+            h_grouped_words = h_grouped[:].bitcast(F32).rearrange(
+                "p (kp g o c u) -> p kp g o c u", kp=H_PASSES, g=G, o=2, u=2
+            )
+            for odd in range(2):
                 nc.scalar.copy(
                     out=h_grouped_words[:, :, :, 1 - odd, :, :],
-                    in_=flipped[:].rearrange("p kp u (g c) -> p kp g c u", g=G),
+                    in_=h_flipped[(pair, odd)][:].rearrange("p kp u (g c) -> p kp g c u", g=G),
                 )
+
+        def quantise_h(pair):
+            h_grouped = h_grouped_kept[pair]
             for kp in range(H_PASSES):
                 for g in range(G):
                     first = h_slot(pair, g, kp) + C
@@ -139,46 +154,49 @@ def tile_flaxpositionwisemoelayer_pb_kernel(tc, h, wo, combined_weights, out):
 
         cw_grouped_now = {}
 
-        def prepare_cw(g, st):
-            if st % 2 == 0:
-                cw_grouped = cw_grouped_pool.tile([P, 2 * HALVES * P * PACK], BF16, align_bytes=64)
-                cw_grouped_now[g] = cw_grouped
+        cw_flipped = {}
+
+        def transpose_cw(g, st):
             flipped = next_bank([P, HALVES, PACK, P], BF16)
+            cw_flipped[(g, st)] = flipped
             for half in range(HALVES):
                 for t in range(PACK):
                     k2 = st * E * C + half * K_PASS + t * P
                     nc.tensor.transpose(
                         flipped[:, half, t, :], cw_raw[g][:, k2 : k2 + P], identity_bf16[:]
                     )
+
+        def copy_cw(g, st):
+            if st % 2 == 0:
+                cw_grouped = cw_grouped_pool.tile([P, 2 * HALVES * P * PACK], BF16, align_bytes=64)
+                cw_grouped_now[(g, st // 2)] = cw_grouped
             values = (st % 2) * HALVES * K_PASS
             nc.scalar.copy(
-                out=cw_grouped_now[g][:, values : values + HALVES * K_PASS].rearrange(
+                out=cw_grouped_now[(g, st // 2)][:, values : values + HALVES * K_PASS].rearrange(
                     "p (half i t) -> p half i t", half=HALVES, t=PACK
                 ),
-                in_=flipped[:].rearrange("p half t i -> p half i t"),
+                in_=cw_flipped[(g, st)][:].rearrange("p half t i -> p half i t"),
             )
+
+        def quantise_cw(g, st):
             if st % 2 == 1:
                 first = (g * S_TILES + st - 1) * HALVES * P
                 nc.vector.quantize_mx(
                     out=cw_words[:, first : first + 2 * HALVES * P].bitcast(FP8X4),
                     scales=cw_scales[:, first : first + 2 * HALVES * P],
-                    in_=cw_grouped_now[g][:],
+                    in_=cw_grouped_now[(g, st // 2)][:],
                 )
 
         wo_mx = {}
 
         wo_grouped_kept = {}
+        wo_kept = {}
 
         def regroup_wo(e, vector_groups):
             wo_grouped = wo_grouped_pool.tile([P, H_PASSES * M * PACK], BF16, align_bytes=64)
             wo_grouped_kept[e] = wo_grouped
             for kp in range(H_PASSES):
-                wo_raw = wo_raw_pool.tile([P, PACK * M], BF16)
-                nc.sync.dma_start(
-                    out=wo_raw[:],
-                    in_=wo[e, kp * K_PASS : (kp + 1) * K_PASS, :].rearrange("(p j) m -> p (j m)", j=PACK),
-                )
-                rows = wo_raw[:].rearrange("p (j c i) -> p c j i", j=PACK, i=4)
+                rows = wo_kept[(e, kp)][:].rearrange("p (j c i) -> p c j i", j=PACK, i=4)
                 columns = wo_grouped[:, kp * M * PACK : (kp + 1) * M * PACK].rearrange(
                     "p (c i j) -> p c j i", i=4, j=PACK
                 )
@@ -195,8 +213,6 @@ def tile_flaxpositionwisemoelayer_pb_kernel(tc, h, wo, combined_weights, out):
             nc.vector.quantize_mx(
                 out=wo_words[:].bitcast(FP8X4), scales=wo_scales[:], in_=wo_grouped_kept[e][:]
             )
-
-        wo_kept = {}
 
         def load_wo(e):
             for kp in range(H_PASSES):
@@ -288,22 +304,38 @@ def tile_flaxpositionwisemoelayer_pb_kernel(tc, h, wo, combined_weights, out):
                 in_=eo_grouped[:],
             )
 
-        for r in range(HALF_EXPERTS):
-            prepare_h(r)
-            regroup_wo(r, VECTOR_GROUPS_EARLY)
-            if r > 0:
-                quantise_wo(r - 1)
+        def load_and_transpose(r):
+            load_h(r)
+            load_wo(r)
             if r % S_TILES == 0:
                 load_cw(r // S_TILES)
-            prepare_cw(r // S_TILES, r % S_TILES)
+            transpose_h(r)
+            transpose_cw(r // S_TILES, r % S_TILES)
+
+        def quantise_round(r):
+            quantise_h(r)
+            quantise_wo(r)
+            quantise_cw(r // S_TILES, r % S_TILES)
+
+        load_and_transpose(0)
+        for r in range(HALF_EXPERTS):
+            if r + 1 < HALF_EXPERTS:
+                load_and_transpose(r + 1)
+            copy_h(r)
+            regroup_wo(r, VECTOR_GROUPS_EARLY)
+            copy_cw(r // S_TILES, r % S_TILES)
+            if r > 0:
+                quantise_round(r - 1)
+        load_wo(HALF_EXPERTS)
         regroup_wo(HALF_EXPERTS, VECTOR_GROUPS_LATE)
-        quantise_wo(HALF_EXPERTS - 1)
+        quantise_round(HALF_EXPERTS - 1)
         for e in range(HALF_EXPERTS):
             first_product(e)
         for g in range(G):
             quantise_eo(0, g, False)
 
         for e in range(HALF_EXPERTS + 1, E - SPLIT_EXPERTS):
+            load_wo(e)
             regroup_wo(e, VECTOR_GROUPS_LATE)
             quantise_wo(e - 1)
             first_product(e - 1)

@@ -317,15 +317,16 @@ def tile_flaxpositionwisemoelayer_pb_kernel(tc, h, wo, combined_weights, out):
             quantise_wo(r)
             quantise_cw(r // S_TILES, r % S_TILES)
 
-        load_and_transpose(0)
-        for r in range(HALF_EXPERTS):
-            if r + 1 < HALF_EXPERTS:
-                load_and_transpose(r + 1)
-            copy_h(r)
-            regroup_wo(r, VECTOR_GROUPS_EARLY)
-            copy_cw(r // S_TILES, r % S_TILES)
-            if r > 0:
-                quantise_round(r - 1)
+        with tc.manual_schedule():
+            load_and_transpose(0)
+            for r in range(HALF_EXPERTS):
+                if r + 1 < HALF_EXPERTS:
+                    load_and_transpose(r + 1)
+                copy_h(r)
+                regroup_wo(r, VECTOR_GROUPS_EARLY)
+                copy_cw(r // S_TILES, r % S_TILES)
+                if r > 0:
+                    quantise_round(r - 1)
         load_wo(HALF_EXPERTS)
         regroup_wo(HALF_EXPERTS, VECTOR_GROUPS_LATE)
         quantise_round(HALF_EXPERTS - 1)

@@ -26,10 +26,10 @@ H_SLOT = 3 * C
 H_SLOTS = PAIRS * G * H_PASSES
 COLUMN_GROUPS = M // 4
 
-VECTOR_GROUPS_EARLY = 40
-VECTOR_GROUPS_LATE = 16
+VECTOR_GROUPS_EARLY = 48
+VECTOR_GROUPS_LATE = 0
 
-SPLIT_EXPERTS = 4
+SPLIT_EXPERTS = 2
 COLUMN_HALVES = 2
 HALF_M = M // COLUMN_HALVES
 HALF_CHUNKS = M_CHUNKS // COLUMN_HALVES
@@ -203,7 +203,8 @@ def tile_flaxpositionwisemoelayer_pb_kernel(tc, h, wo, combined_weights, out):
                 if kp == 0:
                     nc.vector.tensor_copy(out=columns, in_=rows)
                 else:
-                    nc.vector.tensor_copy(out=columns[:, :vector_groups], in_=rows[:, :vector_groups])
+                    if vector_groups > 0:
+                        nc.vector.tensor_copy(out=columns[:, :vector_groups], in_=rows[:, :vector_groups])
                     nc.scalar.copy(out=columns[:, vector_groups:], in_=rows[:, vector_groups:])
 
         def quantise_wo(e):

@@ -21,15 +21,24 @@ PAIRS = E // 2
 M_CHUNK = P
 M_CHUNKS = M // M_CHUNK
 S_TILES = S // P
-BANKS = 8
 H_SLOT = 3 * C
 H_SLOTS = PAIRS * G * H_PASSES
+CW_RUN = 256
+CW_TOKENS = P * CW_RUN // (E * C)
+CW_BLOCKS = P // CW_TOKENS
 COLUMN_GROUPS = M // 4
 
-VECTOR_GROUPS_EARLY = 48
-VECTOR_GROUPS_LATE = 0
+H_STEP = (3, 4, 6, 7, 8, 10, 11, 12)
+CW_STEP = (10, 11, 12, 13)
+EO_STEP = HALF_EXPERTS + 1
+
+VECTOR_GROUPS = 0
+VECTOR_GROUPS_CW = 40
+
+FIRST_CHUNKS = 3
 
 SPLIT_EXPERTS = 2
+WHOLE_EXPERTS = E - SPLIT_EXPERTS
 COLUMN_HALVES = 2
 HALF_M = M // COLUMN_HALVES
 HALF_CHUNKS = M_CHUNKS // COLUMN_HALVES
@@ -48,6 +57,7 @@ def tile_flaxpositionwisemoelayer_pb_kernel(tc, h, wo, combined_weights, out):
     nc = tc.nc
     with ExitStack() as ctx:
         keep = ctx.enter_context(tc.tile_pool(name="keep", bufs=1))
+        cw_raw_pool = ctx.enter_context(tc.tile_pool(name="cw_raw", bufs=3))
         h_raw_pool = ctx.enter_context(tc.tile_pool(name="h_raw", bufs=3))
         wo_raw_pool = ctx.enter_context(tc.tile_pool(name="wo_raw", bufs=8))
         wo_grouped_pool = ctx.enter_context(tc.tile_pool(name="wo_grouped", bufs=3))
@@ -56,18 +66,15 @@ def tile_flaxpositionwisemoelayer_pb_kernel(tc, h, wo, combined_weights, out):
         grouped_pool = ctx.enter_context(tc.tile_pool(name="grouped", bufs=3))
         cw_grouped_pool = ctx.enter_context(tc.tile_pool(name="cw_grouped", bufs=2))
         eo_grouped_pool = ctx.enter_context(tc.tile_pool(name="eo_grouped", bufs=2))
-        result_pool = ctx.enter_context(tc.tile_pool(name="result", bufs=4))
+        result_pool = ctx.enter_context(tc.tile_pool(name="result", bufs=8))
         psum = ctx.enter_context(tc.psum_pool(name="psum", bufs=1))
 
         def bank(index, shape, dtype):
-            tag = "bank%d" % (index % BANKS)
+            tag = "bank%d" % index
             return psum.tile(shape, dtype, name=tag, tag=tag)
 
-        banks_taken = []
-
-        def next_bank(shape, dtype):
-            banks_taken.append(1)
-            return bank(len(banks_taken) - 1, shape, dtype)
+        def unit_bank(g, mc):
+            return mc * G + g
 
         identity_f32 = keep.tile([P, P], F32, name="identity_f32")
         make_identity(nc, identity_f32[:])
@@ -111,7 +118,8 @@ def tile_flaxpositionwisemoelayer_pb_kernel(tc, h, wo, combined_weights, out):
                 "p (e kp w u) -> p e kp u w", e=2, kp=H_PASSES, u=2
             )
             for odd in range(2):
-                flipped = next_bank([P, H_PASSES, 2, P], F32)
+                first_bank = 6 if pair < PAIRS // 2 + 1 else 4
+                flipped = bank(first_bank + odd, [P, H_PASSES, 2, P], F32)
                 h_flipped[(pair, odd)] = flipped
                 for kp in range(H_PASSES):
                     for u in range(2):
@@ -145,11 +153,14 @@ def tile_flaxpositionwisemoelayer_pb_kernel(tc, h, wo, combined_weights, out):
 
         cw_raw = {}
 
-        def load_cw(g):
-            cw_raw[g] = keep.tile([P, S_TILES * E * C], BF16, name="cw_raw%d" % g)
+        def load_cw(g, q):
+            cw_pair = cw_raw_pool.tile([P, 2 * E * C], BF16)
+            cw_raw[(g, q)] = cw_pair
             nc.sync.dma_start(
-                out=cw_raw[g][:],
-                in_=combined_weights[g].rearrange("(i st) e c -> i (st e c)", st=S_TILES),
+                out=cw_pair[:].rearrange("p (block v) -> p block v", v=CW_RUN),
+                in_=combined_weights[g, q * 2 * P : (q + 1) * 2 * P].rearrange(
+                    "(block i) (r x) c -> (i r) block (x c)", i=CW_TOKENS, r=E * C // CW_RUN
+                ),
             )
 
         cw_grouped_now = {}
@@ -157,13 +168,13 @@ def tile_flaxpositionwisemoelayer_pb_kernel(tc, h, wo, combined_weights, out):
         cw_flipped = {}
 
         def transpose_cw(g, st):
-            flipped = next_bank([P, HALVES, PACK, P], BF16)
+            flipped = bank(6 + st % 2, [P, CW_BLOCKS, 2, P], BF16)
             cw_flipped[(g, st)] = flipped
-            for half in range(HALVES):
-                for t in range(PACK):
-                    k2 = st * E * C + half * K_PASS + t * P
+            for block in range(CW_BLOCKS):
+                for b in range(2):
+                    first = (st % 2 * CW_BLOCKS + block) * CW_RUN + b * P
                     nc.tensor.transpose(
-                        flipped[:, half, t, :], cw_raw[g][:, k2 : k2 + P], identity_bf16[:]
+                        flipped[:, block, b, :], cw_raw[(g, st // 2)][:, first : first + P], identity_bf16[:]
                     )
 
         def copy_cw(g, st):
@@ -172,10 +183,12 @@ def tile_flaxpositionwisemoelayer_pb_kernel(tc, h, wo, combined_weights, out):
                 cw_grouped_now[(g, st // 2)] = cw_grouped
             values = (st % 2) * HALVES * K_PASS
             nc.scalar.copy(
-                out=cw_grouped_now[(g, st // 2)][:, values : values + HALVES * K_PASS].rearrange(
-                    "p (half i t) -> p half i t", half=HALVES, t=PACK
+                out=cw_grouped_now[(g, st // 2)][:, values : values + HALVES * K_PASS].bitcast(F32).rearrange(
+                    "p (half block i b) -> p half block i b", half=HALVES, block=CW_BLOCKS, b=2
                 ),
-                in_=cw_flipped[(g, st)][:].rearrange("p half t i -> p half i t"),
+                in_=cw_flipped[(g, st)][:].rearrange("p block b w -> p (block b w)").bitcast(F32).rearrange(
+                    "p (block b i half) -> p half block i b", block=CW_BLOCKS, b=2, half=HALVES
+                ),
             )
 
         def quantise_cw(g, st):
@@ -245,8 +258,11 @@ def tile_flaxpositionwisemoelayer_pb_kernel(tc, h, wo, combined_weights, out):
 
         eo_banks = {}
 
+        def word_place(pair_of_half):
+            return 2 * (pair_of_half % 2) + pair_of_half // 2
+
         def first_product_columns(e, ch):
-            t = (e % HALF_EXPERTS) // 2
+            t = word_place((e % HALF_EXPERTS) // 2)
             odd = e % 2
             wo_words, wo_scales = wo_mx[(e, ch)]
             for kp in range(H_PASSES):
@@ -264,18 +280,18 @@ def tile_flaxpositionwisemoelayer_pb_kernel(tc, h, wo, combined_weights, out):
                             stop=(odd == 1 and kp == H_PASSES - 1),
                         )
 
-        def first_product(e):
-            t = (e % HALF_EXPERTS) // 2
+        def first_product(e, chunks):
+            t = word_place((e % HALF_EXPERTS) // 2)
             odd = e % 2
             if e % HALF_EXPERTS == 0:
-                for g in range(G):
-                    for mc in range(M_CHUNKS):
-                        eo_banks[(g, mc)] = bank(g * M_CHUNKS + mc, [P, PACK, M_CHUNK], F32)
+                for mc in chunks:
+                    for g in range(G):
+                        eo_banks[(g, mc)] = bank(unit_bank(g, mc), [P, PACK, M_CHUNK], F32)
             wo_words, wo_scales = wo_mx[e]
             for kp in range(H_PASSES):
                 for g in range(G):
                     window = h_slot(e // 2, g, kp) + (1 - odd) * 2 * C
-                    for mc in range(M_CHUNKS):
+                    for mc in chunks:
                         cols = kp * M + mc * M_CHUNK
                         nc.tensor.matmul_mx(
                             out=eo_banks[(g, mc)][:, t, :],
@@ -287,67 +303,83 @@ def tile_flaxpositionwisemoelayer_pb_kernel(tc, h, wo, combined_weights, out):
                             stop=(odd == 1 and kp == H_PASSES - 1),
                         )
 
-        def quantise_eo(half, g, both_engines):
-            eo_grouped = eo_grouped_pool.tile([P, M * PACK], BF16, align_bytes=64)
-            for mc in range(M_CHUNKS):
-                copy_by_turns(
-                    nc,
-                    mc if both_engines else 1,
-                    out=eo_grouped[:, mc * K_PASS : (mc + 1) * K_PASS].rearrange(
-                        "p (m t) -> p m t", t=PACK
-                    ),
-                    in_=eo_banks[(g, mc)][:].rearrange("p t m -> p m t"),
-                )
-            first = (half * G + g) * M
-            nc.vector.quantize_mx(
-                out=eo_words[:, first : first + M].bitcast(FP8X4),
-                scales=eo_scales[:, first : first + M],
-                in_=eo_grouped[:],
-            )
+        eo_grouped_first = {}
 
-        def load_and_transpose(r):
-            load_h(r)
-            load_wo(r)
-            if r % S_TILES == 0:
-                load_cw(r // S_TILES)
-            transpose_h(r)
-            transpose_cw(r // S_TILES, r % S_TILES)
-
-        def quantise_round(r):
-            quantise_h(r)
-            quantise_wo(r)
-            quantise_cw(r // S_TILES, r % S_TILES)
-
-        with tc.manual_schedule():
-            load_and_transpose(0)
-            for r in range(HALF_EXPERTS):
-                if r + 1 < HALF_EXPERTS:
-                    load_and_transpose(r + 1)
-                copy_h(r)
-                regroup_wo(r, VECTOR_GROUPS_EARLY)
-                copy_cw(r // S_TILES, r % S_TILES)
-                if r > 0:
-                    quantise_round(r - 1)
-        load_wo(HALF_EXPERTS)
-        regroup_wo(HALF_EXPERTS, VECTOR_GROUPS_LATE)
-        quantise_round(HALF_EXPERTS - 1)
-        for e in range(HALF_EXPERTS):
-            first_product(e)
-        for g in range(G):
-            quantise_eo(0, g, False)
-
-        for e in range(HALF_EXPERTS + 1, E - SPLIT_EXPERTS):
-            load_wo(e)
-            regroup_wo(e, VECTOR_GROUPS_LATE)
-            quantise_wo(e - 1)
-            first_product(e - 1)
-        for e in range(E - SPLIT_EXPERTS, E):
-            load_wo(e)
-
-        out_rows = out.rearrange("g (i st) m -> i g st m", st=S_TILES)
-        def finish_columns(ch):
+        def copy_first_eo():
             for g in range(G):
                 eo_grouped = eo_grouped_pool.tile([P, M * PACK], BF16, align_bytes=64)
+                eo_grouped_first[g] = eo_grouped
+            for mc in range(M_CHUNKS):
+                for g in range(G):
+                    out = eo_grouped_first[g][:, mc * K_PASS : (mc + 1) * K_PASS].rearrange(
+                        "p (m t) -> p m t", t=PACK
+                    )
+                    in_ = eo_banks[(g, mc)][:].rearrange("p t m -> p m t")
+                    copy_by_turns(nc, 0 if g == 1 and mc >= 2 else 1, out=out, in_=in_)
+
+        def quantise_first_eo():
+            for g in range(G):
+                nc.vector.quantize_mx(
+                    out=eo_words[:, g * M : (g + 1) * M].bitcast(FP8X4),
+                    scales=eo_scales[:, g * M : (g + 1) * M],
+                    in_=eo_grouped_first[g][:],
+                )
+
+        def cw_tiles(j):
+            return [(j // 2, 2 * (j % 2) + x) for x in range(2)]
+
+        def load_step(r):
+            load_wo(r)
+            for pair in range(PAIRS):
+                if H_STEP[pair] == r:
+                    load_h(pair)
+            for j in range(len(CW_STEP)):
+                if CW_STEP[j] == r:
+                    load_cw(j // 2, j % 2)
+
+        def transpose_step(r):
+            for pair in range(PAIRS):
+                if H_STEP[pair] == r:
+                    transpose_h(pair)
+            for j in range(len(CW_STEP)):
+                if CW_STEP[j] == r:
+                    for g, st in cw_tiles(j):
+                        transpose_cw(g, st)
+
+        def copy_step(r):
+            for pair in range(PAIRS):
+                if H_STEP[pair] == r:
+                    copy_h(pair)
+            for j in range(len(CW_STEP)):
+                if CW_STEP[j] == r:
+                    for g, st in cw_tiles(j):
+                        copy_cw(g, st)
+
+        products_done = []
+
+        def quantise_step(r):
+            for pair in range(PAIRS):
+                if H_STEP[pair] == r:
+                    quantise_h(pair)
+            for j in range(len(CW_STEP)):
+                if CW_STEP[j] == r:
+                    quantise_cw(j // 2, 2 * (j % 2) + 1)
+            quantise_wo(r)
+
+        def multiply_step(r):
+            for e in range(len(products_done), r + 1):
+                if H_STEP[e // 2] <= r:
+                    products_done.append(e)
+                    first_product(e, range(FIRST_CHUNKS if e < HALF_EXPERTS else HALF_CHUNKS))
+
+        out_rows = out.rearrange("g (st i) m -> i g st m", st=S_TILES)
+        eo_grouped_columns = {}
+        accs = {}
+
+        def copy_eo_columns(ch):
+            for g in range(G):
+                eo_grouped = eo_grouped_pool.tile([P, M * PACK], BF16, align_bytes=64)
+                eo_grouped_columns[(ch, g)] = eo_grouped
                 for c2 in range(HALF_CHUNKS):
                     copy_by_turns(
                         nc,
@@ -357,15 +389,21 @@ def tile_flaxpositionwisemoelayer_pb_kernel(tc, h, wo, combined_weights, out):
                         ),
                         in_=eo_banks[(g, ch * HALF_CHUNKS + c2)][:].rearrange("p t m -> p m t"),
                     )
+
+        def quantise_eo_columns(ch):
+            for g in range(G):
                 first = (G + g) * M + ch * HALF_M
                 nc.vector.quantize_mx(
                     out=eo_words[:, first : first + HALF_M].bitcast(FP8X4),
                     scales=eo_scales[:, first : first + HALF_M],
-                    in_=eo_grouped[:, : HALF_M * PACK],
+                    in_=eo_grouped_columns[(ch, g)][:, : HALF_M * PACK],
                 )
+
+        def second_product_columns(ch):
             for g in range(G):
                 for q in range(S_TILES // 2):
-                    acc = bank(g * M_CHUNKS + ch * HALF_CHUNKS + q, [P, 2, HALF_M], F32)
+                    acc = bank(unit_bank(g, ch * HALF_CHUNKS + q), [P, 2, HALF_M], F32)
+                    accs[(ch, g, q)] = acc
                     for s2 in range(2):
                         st = 2 * q + s2
                         for half in range(HALVES):
@@ -380,20 +418,52 @@ def tile_flaxpositionwisemoelayer_pb_kernel(tc, h, wo, combined_weights, out):
                                 start=(half == 0),
                                 stop=(half == HALVES - 1),
                             )
+
+        def store_columns(ch):
+            for g in range(G):
+                for q in range(S_TILES // 2):
                     result = result_pool.tile([P, 2, HALF_M], F32)
-                    copy_by_turns(nc, q, out=result[:], in_=acc[:])
+                    copy_by_turns(nc, q, out=result[:], in_=accs[(ch, g, q)][:])
                     nc.sync.dma_start(
                         out=out_rows[:, g, 2 * q : 2 * q + 2, ch * HALF_M : (ch + 1) * HALF_M], in_=result[:]
                     )
 
-        regroup_wo_columns(E - SPLIT_EXPERTS, 0)
-        quantise_wo(E - SPLIT_EXPERTS - 1)
-        first_product(E - SPLIT_EXPERTS - 1)
-        pieces = [(e, ch) for ch in range(COLUMN_HALVES) for e in range(E - SPLIT_EXPERTS, E)]
-        for i in range(len(pieces)):
-            if i + 1 < len(pieces):
-                regroup_wo_columns(pieces[i + 1][0], pieces[i + 1][1])
-            quantise_wo_columns(pieces[i][0], pieces[i][1])
-            first_product_columns(pieces[i][0], pieces[i][1])
-            if pieces[i][0] == E - 1:
-                finish_columns(pieces[i][1])
+        with tc.manual_schedule():
+            for r in range(WHOLE_EXPERTS):
+                load_step(r)
+                transpose_step(r)
+                regroup_wo(r, VECTOR_GROUPS_CW if r in CW_STEP else VECTOR_GROUPS)
+                copy_step(r)
+                if r > 0:
+                    quantise_step(r - 1)
+                if r == EO_STEP:
+                    copy_first_eo()
+                if r == EO_STEP + 1:
+                    quantise_first_eo()
+                if r > 0:
+                    multiply_step(r - 1)
+                if r == HALF_EXPERTS:
+                    for e in range(HALF_EXPERTS):
+                        first_product(e, range(FIRST_CHUNKS, M_CHUNKS))
+            for e in range(HALF_EXPERTS, WHOLE_EXPERTS - 1):
+                first_product(e, range(HALF_CHUNKS, M_CHUNKS))
+            for e in range(WHOLE_EXPERTS, E):
+                load_wo(e)
+
+            regroup_wo_columns(WHOLE_EXPERTS, 0)
+            quantise_step(WHOLE_EXPERTS - 1)
+            first_product(WHOLE_EXPERTS - 1, range(M_CHUNKS))
+            pieces = [(e, ch) for ch in range(COLUMN_HALVES) for e in range(WHOLE_EXPERTS, E)]
+            for i in range(len(pieces)):
+                if i + 1 < len(pieces):
+                    regroup_wo_columns(pieces[i + 1][0], pieces[i + 1][1])
+                quantise_wo_columns(pieces[i][0], pieces[i][1])
+                first_product_columns(pieces[i][0], pieces[i][1])
+            copy_eo_columns(0)
+            quantise_eo_columns(0)
+            second_product_columns(0)
+            copy_eo_columns(1)
+            quantise_eo_columns(1)
+            second_product_columns(1)
+            store_columns(0)
+            store_columns(1)

@@ -32,10 +32,12 @@ H_STEP = (3, 4, 6, 7, 8, 10, 11, 12)
 CW_STEP = (10, 11, 12, 13)
 EO_STEP = HALF_EXPERTS + 1
 
-VECTOR_GROUPS = 0
-VECTOR_GROUPS_CW = 40
+VECTOR_GROUPS_A_BANK = 12
 
-FIRST_CHUNKS = 3
+CHUNK_STEPS = (
+    (((0, 1, 2), 0), ((3,), 7)),
+    (((0, 1), 8), ((2,), 12), ((3,), 13)),
+)
 
 SPLIT_EXPERTS = 2
 WHOLE_EXPERTS = E - SPLIT_EXPERTS
@@ -46,8 +48,8 @@ HALF_CHUNKS = M_CHUNKS // COLUMN_HALVES
 FLOPS = 2 * E * G * C * H * M + 2 * G * S * E * C * M
 
 
-def copy_by_turns(nc, piece, out, in_):
-    if piece % 2 == 0:
+def copy_out(nc, on_vector, out, in_):
+    if on_vector:
         nc.vector.tensor_copy(out=out, in_=in_)
     else:
         nc.scalar.copy(out=out, in_=in_)
@@ -246,7 +248,7 @@ def tile_flaxpositionwisemoelayer_pb_kernel(tc, h, wo, combined_weights, out):
                 columns = wo_grouped[:, kp * HALF_M * PACK : (kp + 1) * HALF_M * PACK].rearrange(
                     "p (c i j) -> p c j i", i=4, j=PACK
                 )
-                copy_by_turns(nc, kp, out=columns, in_=rows[:, ch * groups : (ch + 1) * groups])
+                copy_out(nc, kp == 0, out=columns, in_=rows[:, ch * groups : (ch + 1) * groups])
 
         def quantise_wo_columns(e, ch):
             wo_words = wo_mx_cols_pool.tile([P, H_PASSES * HALF_M], U32, align_bytes=64)
@@ -315,7 +317,7 @@ def tile_flaxpositionwisemoelayer_pb_kernel(tc, h, wo, combined_weights, out):
                         "p (m t) -> p m t", t=PACK
                     )
                     in_ = eo_banks[(g, mc)][:].rearrange("p t m -> p m t")
-                    copy_by_turns(nc, 0 if g == 1 and mc >= 2 else 1, out=out, in_=in_)
+                    copy_out(nc, g == 1 and mc >= 2, out=out, in_=in_)
 
         def quantise_first_eo():
             for g in range(G):
@@ -355,8 +357,6 @@ def tile_flaxpositionwisemoelayer_pb_kernel(tc, h, wo, combined_weights, out):
                     for g, st in cw_tiles(j):
                         copy_cw(g, st)
 
-        products_done = []
-
         def quantise_step(r):
             for pair in range(PAIRS):
                 if H_STEP[pair] == r:
@@ -366,24 +366,32 @@ def tile_flaxpositionwisemoelayer_pb_kernel(tc, h, wo, combined_weights, out):
                     quantise_cw(j // 2, 2 * (j % 2) + 1)
             quantise_wo(r)
 
+        multiplied = {}
+
         def multiply_step(r):
-            for e in range(len(products_done), r + 1):
-                if H_STEP[e // 2] <= r:
-                    products_done.append(e)
-                    first_product(e, range(FIRST_CHUNKS if e < HALF_EXPERTS else HALF_CHUNKS))
+            for half in range(HALVES):
+                for chunks, first_step in CHUNK_STEPS[half]:
+                    waiting = range(multiplied.get((half, chunks), half * HALF_EXPERTS), (half + 1) * HALF_EXPERTS)
+                    for e in waiting:
+                        if first_step <= r and e <= r and H_STEP[e // 2] <= r:
+                            first_product(e, chunks)
+                            multiplied[(half, chunks)] = e + 1
 
         out_rows = out.rearrange("g (st i) m -> i g st m", st=S_TILES)
         eo_grouped_columns = {}
         accs = {}
+
+        def vector_empties(ch, g, i):
+            return i == 0 and not (ch == 0 and g == 0)
 
         def copy_eo_columns(ch):
             for g in range(G):
                 eo_grouped = eo_grouped_pool.tile([P, M * PACK], BF16, align_bytes=64)
                 eo_grouped_columns[(ch, g)] = eo_grouped
                 for c2 in range(HALF_CHUNKS):
-                    copy_by_turns(
+                    copy_out(
                         nc,
-                        c2,
+                        vector_empties(ch, g, c2),
                         out=eo_grouped[:, c2 * K_PASS : (c2 + 1) * K_PASS].rearrange(
                             "p (m t) -> p m t", t=PACK
                         ),
@@ -423,7 +431,7 @@ def tile_flaxpositionwisemoelayer_pb_kernel(tc, h, wo, combined_weights, out):
             for g in range(G):
                 for q in range(S_TILES // 2):
                     result = result_pool.tile([P, 2, HALF_M], F32)
-                    copy_by_turns(nc, q, out=result[:], in_=accs[(ch, g, q)][:])
+                    copy_out(nc, vector_empties(ch, g, q), out=result[:], in_=accs[(ch, g, q)][:])
                     nc.sync.dma_start(
                         out=out_rows[:, g, 2 * q : 2 * q + 2, ch * HALF_M : (ch + 1) * HALF_M], in_=result[:]
                     )
@@ -432,7 +440,7 @@ def tile_flaxpositionwisemoelayer_pb_kernel(tc, h, wo, combined_weights, out):
             for r in range(WHOLE_EXPERTS):
                 load_step(r)
                 transpose_step(r)
-                regroup_wo(r, VECTOR_GROUPS_CW if r in CW_STEP else VECTOR_GROUPS)
+                regroup_wo(r, VECTOR_GROUPS_A_BANK * 2 * (H_STEP.count(r) + CW_STEP.count(r)))
                 copy_step(r)
                 if r > 0:
                     quantise_step(r - 1)
@@ -442,17 +450,12 @@ def tile_flaxpositionwisemoelayer_pb_kernel(tc, h, wo, combined_weights, out):
                     quantise_first_eo()
                 if r > 0:
                     multiply_step(r - 1)
-                if r == HALF_EXPERTS:
-                    for e in range(HALF_EXPERTS):
-                        first_product(e, range(FIRST_CHUNKS, M_CHUNKS))
-            for e in range(HALF_EXPERTS, WHOLE_EXPERTS - 1):
-                first_product(e, range(HALF_CHUNKS, M_CHUNKS))
             for e in range(WHOLE_EXPERTS, E):
                 load_wo(e)
 
             regroup_wo_columns(WHOLE_EXPERTS, 0)
             quantise_step(WHOLE_EXPERTS - 1)
-            first_product(WHOLE_EXPERTS - 1, range(M_CHUNKS))
+            multiply_step(WHOLE_EXPERTS - 1)
             pieces = [(e, ch) for ch in range(COLUMN_HALVES) for e in range(WHOLE_EXPERTS, E)]
             for i in range(len(pieces)):
                 if i + 1 < len(pieces):

@@ -29,14 +29,14 @@ CW_BLOCKS = P // CW_TOKENS
 COLUMN_GROUPS = M // 4
 
 H_STEP = (3, 4, 6, 7, 8, 10, 11, 12)
-CW_STEP = (10, 11, 12, 13)
+CW_STEP = (2, 5, 10, 11)
 EO_STEP = HALF_EXPERTS + 1
 
 VECTOR_GROUPS_A_BANK = 12
 
 CHUNK_STEPS = (
     (((0, 1, 2), 0), ((3,), 7)),
-    (((0, 1), 8), ((2,), 12), ((3,), 13)),
+    (((0, 1), 8), ((3,), 11), ((2,), 12)),
 )
 
 SPLIT_EXPERTS = 2
@@ -317,7 +317,7 @@ def tile_flaxpositionwisemoelayer_pb_kernel(tc, h, wo, combined_weights, out):
                         "p (m t) -> p m t", t=PACK
                     )
                     in_ = eo_banks[(g, mc)][:].rearrange("p t m -> p m t")
-                    copy_out(nc, g == 1 and mc >= 2, out=out, in_=in_)
+                    copy_out(nc, g == 1 and mc < 2, out=out, in_=in_)
 
         def quantise_first_eo():
             for g in range(G):

@@ -32,7 +32,7 @@ H_STEP = (3, 4, 6, 7, 8, 10, 11, 12)
 CW_STEP = (2, 5, 10, 11)
 EO_STEP = HALF_EXPERTS + 1
 
-VECTOR_GROUPS_A_BANK = 12
+VECTOR_GROUPS_A_BANK = 4
 
 CHUNK_STEPS = (
     (((0, 1, 2), 0), ((3,), 7)),
@@ -61,7 +61,7 @@ def tile_flaxpositionwisemoelayer_pb_kernel(tc, h, wo, combined_weights, out):
         keep = ctx.enter_context(tc.tile_pool(name="keep", bufs=1))
         cw_raw_pool = ctx.enter_context(tc.tile_pool(name="cw_raw", bufs=3))
         h_raw_pool = ctx.enter_context(tc.tile_pool(name="h_raw", bufs=3))
-        wo_raw_pool = ctx.enter_context(tc.tile_pool(name="wo_raw", bufs=8))
+        wo_raw_pool = ctx.enter_context(tc.tile_pool(name="wo_raw", bufs=4))
         wo_grouped_pool = ctx.enter_context(tc.tile_pool(name="wo_grouped", bufs=3))
         wo_mx_pool = ctx.enter_context(tc.tile_pool(name="wo_mx", bufs=HALF_EXPERTS + 2))
         wo_mx_cols_pool = ctx.enter_context(tc.tile_pool(name="wo_mx_cols", bufs=4))
@@ -207,20 +207,18 @@ def tile_flaxpositionwisemoelayer_pb_kernel(tc, h, wo, combined_weights, out):
         wo_grouped_kept = {}
         wo_kept = {}
 
-        def regroup_wo(e, vector_groups):
+        def regroup_wo(e, banks):
             wo_grouped = wo_grouped_pool.tile([P, H_PASSES * M * PACK], BF16, align_bytes=64)
             wo_grouped_kept[e] = wo_grouped
-            for kp in range(H_PASSES):
-                rows = wo_kept[(e, kp)][:].rearrange("p (j c i) -> p c j i", j=PACK, i=4)
-                columns = wo_grouped[:, kp * M * PACK : (kp + 1) * M * PACK].rearrange(
-                    "p (c i j) -> p c j i", i=4, j=PACK
-                )
-                if kp == 0:
-                    nc.vector.tensor_copy(out=columns, in_=rows)
-                else:
-                    if vector_groups > 0:
-                        nc.vector.tensor_copy(out=columns[:, :vector_groups], in_=rows[:, :vector_groups])
-                    nc.scalar.copy(out=columns[:, vector_groups:], in_=rows[:, vector_groups:])
+            rows = wo_kept[e][:].rearrange("p kp (j c i) -> p kp c j i", j=PACK, i=4)
+            columns = wo_grouped[:].rearrange("p (kp c i j) -> p kp c j i", kp=H_PASSES, i=4, j=PACK)
+            if banks == 0:
+                nc.vector.tensor_copy(out=columns[:, 0], in_=rows[:, 0])
+                nc.scalar.copy(out=columns[:, 1], in_=rows[:, 1])
+            else:
+                share = COLUMN_GROUPS // 2 + VECTOR_GROUPS_A_BANK * banks
+                nc.vector.tensor_copy(out=columns[:, :, :share], in_=rows[:, :, :share])
+                nc.scalar.copy(out=columns[:, :, share:], in_=rows[:, :, share:])
 
         def quantise_wo(e):
             wo_words = wo_mx_pool.tile([P, H_PASSES * M], U32, align_bytes=64)
@@ -231,20 +229,20 @@ def tile_flaxpositionwisemoelayer_pb_kernel(tc, h, wo, combined_weights, out):
             )
 
         def load_wo(e):
+            wo_raw = wo_raw_pool.tile([P, H_PASSES, PACK * M], BF16)
+            wo_kept[e] = wo_raw
             for kp in range(H_PASSES):
-                wo_raw = wo_raw_pool.tile([P, PACK * M], BF16)
                 nc.sync.dma_start(
-                    out=wo_raw[:],
+                    out=wo_raw[:, kp, :],
                     in_=wo[e, kp * K_PASS : (kp + 1) * K_PASS, :].rearrange("(p j) m -> p (j m)", j=PACK),
                 )
-                wo_kept[(e, kp)] = wo_raw
 
         def regroup_wo_columns(e, ch):
             wo_grouped = wo_grouped_pool.tile([P, H_PASSES * HALF_M * PACK], BF16, align_bytes=64)
             wo_grouped_kept[(e, ch)] = wo_grouped
             groups = HALF_M // 4
             for kp in range(H_PASSES):
-                rows = wo_kept[(e, kp)][:].rearrange("p (j c i) -> p c j i", j=PACK, i=4)
+                rows = wo_kept[e][:, kp, :].rearrange("p (j c i) -> p c j i", j=PACK, i=4)
                 columns = wo_grouped[:, kp * HALF_M * PACK : (kp + 1) * HALF_M * PACK].rearrange(
                     "p (c i j) -> p c j i", i=4, j=PACK
                 )
@@ -440,7 +438,7 @@ def tile_flaxpositionwisemoelayer_pb_kernel(tc, h, wo, combined_weights, out):
             for r in range(WHOLE_EXPERTS):
                 load_step(r)
                 transpose_step(r)
-                regroup_wo(r, VECTOR_GROUPS_A_BANK * 2 * (H_STEP.count(r) + CW_STEP.count(r)))
+                regroup_wo(r, 2 * (H_STEP.count(r) + CW_STEP.count(r)))
                 copy_step(r)
                 if r > 0:
                     quantise_step(r - 1)

@@ -34,6 +34,8 @@ EO_STEP = HALF_EXPERTS + 1
 
 VECTOR_GROUPS_A_BANK = 4
 
+WO_LOADS_AHEAD = 4
+
 CHUNK_STEPS = (
     (((0, 1, 2), 0), ((3,), 7)),
     (((0, 1), 8), ((3,), 11), ((2,), 12)),
@@ -231,11 +233,12 @@ def tile_flaxpositionwisemoelayer_pb_kernel(tc, h, wo, combined_weights, out):
         def load_wo(e):
             wo_raw = wo_raw_pool.tile([P, H_PASSES, PACK * M], BF16)
             wo_kept[e] = wo_raw
-            for kp in range(H_PASSES):
-                nc.sync.dma_start(
-                    out=wo_raw[:, kp, :],
-                    in_=wo[e, kp * K_PASS : (kp + 1) * K_PASS, :].rearrange("(p j) m -> p (j m)", j=PACK),
-                )
+            rows = wo[e].rearrange("(kp p j) m -> p kp (j m)", kp=H_PASSES, j=PACK)
+            if e < WO_LOADS_AHEAD:
+                for kp in range(H_PASSES):
+                    nc.sync.dma_start(out=wo_raw[:, kp, :], in_=rows[:, kp, :])
+            else:
+                nc.sync.dma_start(out=wo_raw[:], in_=rows)
 
         def regroup_wo_columns(e, ch):
             wo_grouped = wo_grouped_pool.tile([P, H_PASSES * HALF_M * PACK], BF16, align_bytes=64)
@@ -265,8 +268,8 @@ def tile_flaxpositionwisemoelayer_pb_kernel(tc, h, wo, combined_weights, out):
             t = word_place((e % HALF_EXPERTS) // 2)
             odd = e % 2
             wo_words, wo_scales = wo_mx[(e, ch)]
-            for kp in range(H_PASSES):
-                for g in range(G):
+            for g in range(G):
+                for kp in range(H_PASSES):
                     window = h_slot(e // 2, g, kp) + (1 - odd) * 2 * C
                     for c2 in range(HALF_CHUNKS):
                         cols = kp * HALF_M + c2 * M_CHUNK
@@ -315,7 +318,7 @@ def tile_flaxpositionwisemoelayer_pb_kernel(tc, h, wo, combined_weights, out):
                         "p (m t) -> p m t", t=PACK
                     )
                     in_ = eo_banks[(g, mc)][:].rearrange("p t m -> p m t")
-                    copy_out(nc, g == 1 and mc < 2, out=out, in_=in_)
+                    copy_out(nc, g == 1 and mc < 1, out=out, in_=in_)
 
         def quantise_first_eo():
             for g in range(G):
@@ -367,13 +370,19 @@ def tile_flaxpositionwisemoelayer_pb_kernel(tc, h, wo, combined_weights, out):
         multiplied = {}
 
         def multiply_step(r):
+            def multiply_waiting(half, chunks, first_step, experts):
+                for e in experts:
+                    if e == multiplied.get((half, chunks), half * HALF_EXPERTS) and H_STEP[e // 2] <= r >= first_step:
+                        first_product(e, chunks)
+                        multiplied[(half, chunks)] = e + 1
+
             for half in range(HALVES):
+                experts = range(half * HALF_EXPERTS, min(r + 1, (half + 1) * HALF_EXPERTS))
+                if half == 1:
+                    for chunks, first_step in CHUNK_STEPS[half]:
+                        multiply_waiting(half, chunks, first_step, experts[:-1])
                 for chunks, first_step in CHUNK_STEPS[half]:
-                    waiting = range(multiplied.get((half, chunks), half * HALF_EXPERTS), (half + 1) * HALF_EXPERTS)
-                    for e in waiting:
-                        if first_step <= r and e <= r and H_STEP[e // 2] <= r:
-                            first_product(e, chunks)
-                            multiplied[(half, chunks)] = e + 1
+                    multiply_waiting(half, chunks, first_step, experts)
 
         out_rows = out.rearrange("g (st i) m -> i g st m", st=S_TILES)
         eo_grouped_columns = {}

@@ -29,7 +29,7 @@ CW_BLOCKS = P // CW_TOKENS
 COLUMN_GROUPS = M // 4
 
 H_STEP = (3, 4, 6, 7, 8, 10, 11, 12)
-CW_STEP = (2, 5, 10, 11)
+CW_STEP = (5, 10, 11, 12)
 EO_STEP = HALF_EXPERTS + 1
 
 VECTOR_GROUPS_A_BANK = 4
@@ -38,7 +38,7 @@ WO_LOADS_AHEAD = 4
 
 CHUNK_STEPS = (
     (((0, 1, 2), 0), ((3,), 7)),
-    (((0, 1), 8), ((3,), 11), ((2,), 12)),
+    (((0, 1), 8), ((2, 3), 12)),
 )
 
 SPLIT_EXPERTS = 2

@@ -318,7 +318,7 @@ def tile_flaxpositionwisemoelayer_pb_kernel(tc, h, wo, combined_weights, out):
                         "p (m t) -> p m t", t=PACK
                     )
                     in_ = eo_banks[(g, mc)][:].rearrange("p t m -> p m t")
-                    copy_out(nc, g == 1 and mc < 1, out=out, in_=in_)
+                    nc.scalar.copy(out=out, in_=in_)
 
         def quantise_first_eo():
             for g in range(G):
@@ -339,6 +339,9 @@ def tile_flaxpositionwisemoelayer_pb_kernel(tc, h, wo, combined_weights, out):
             for j in range(len(CW_STEP)):
                 if CW_STEP[j] == r:
                     load_cw(j // 2, j % 2)
+
+        def banks_emptied(r):
+            return 2 * (H_STEP.count(r) + CW_STEP.count(r)) + (G * M_CHUNKS if r == EO_STEP else 0)
 
         def transpose_step(r):
             for pair in range(PAIRS):
@@ -447,7 +450,7 @@ def tile_flaxpositionwisemoelayer_pb_kernel(tc, h, wo, combined_weights, out):
             for r in range(WHOLE_EXPERTS):
                 load_step(r)
                 transpose_step(r)
-                regroup_wo(r, 2 * (H_STEP.count(r) + CW_STEP.count(r)))
+                regroup_wo(r, banks_emptied(r))
                 copy_step(r)
                 if r > 0:
                     quantise_step(r - 1)

from contextlib import ExitStack

import concourse.mybir as mybir
from concourse.masks import make_identity

BF16 = mybir.dt.bfloat16
F32 = mybir.dt.float32
I32 = mybir.dt.int32
U32 = mybir.dt.uint32
U8 = mybir.dt.uint8
FP8X4 = mybir.dt.float8_e4m3fn_x4

G, S, M, H, E, C = 2, 512, 512, 1024, 16, 64
P = 128
PACK = 4
K_PASS = P * PACK
H_PASSES = H // K_PASS
HALVES = E * C // K_PASS
HALF_EXPERTS = E // HALVES
PAIRS = E // 2
M_CHUNK = P
M_CHUNKS = M // M_CHUNK
S_TILES = S // P
H_SLOT = 3 * C
H_SLOTS = PAIRS * G * H_PASSES
CW_RUN = 256
CW_TOKENS = P * CW_RUN // (E * C)
CW_BLOCKS = P // CW_TOKENS
COLUMN_GROUPS = M // 4

H_STEP = (3, 4, 6, 7, 8, 10, 11, 12)
CW_STEP = (5, 10, 11, 12)
EO_STEP = HALF_EXPERTS + 1

VECTOR_GROUPS_A_BANK = 4

WO_LOADS_AHEAD = 4

CHUNK_STEPS = (
    (((0, 1, 2), 0), ((3,), 7)),
    (((0, 1), 8), ((2, 3), 12)),
)

SPLIT_EXPERTS = 2
WHOLE_EXPERTS = E - SPLIT_EXPERTS
COLUMN_HALVES = 2
HALF_M = M // COLUMN_HALVES
HALF_CHUNKS = M_CHUNKS // COLUMN_HALVES

FLOPS = 2 * E * G * C * H * M + 2 * G * S * E * C * M


def copy_out(nc, on_vector, out, in_):
    if on_vector:
        nc.vector.tensor_copy(out=out, in_=in_)
    else:
        nc.scalar.copy(out=out, in_=in_)


def tile_flaxpositionwisemoelayer_pb_kernel(tc, h, wo, combined_weights, out):
    nc = tc.nc
    with ExitStack() as ctx:
        keep = ctx.enter_context(tc.tile_pool(name="keep", bufs=1))
        cw_raw_pool = ctx.enter_context(tc.tile_pool(name="cw_raw", bufs=3))
        h_raw_pool = ctx.enter_context(tc.tile_pool(name="h_raw", bufs=3))
        wo_raw_pool = ctx.enter_context(tc.tile_pool(name="wo_raw", bufs=4))
        wo_grouped_pool = ctx.enter_context(tc.tile_pool(name="wo_grouped", bufs=3))
        wo_mx_pool = ctx.enter_context(tc.tile_pool(name="wo_mx", bufs=HALF_EXPERTS + 2))
        wo_mx_cols_pool = ctx.enter_context(tc.tile_pool(name="wo_mx_cols", bufs=4))
        grouped_pool = ctx.enter_context(tc.tile_pool(name="grouped", bufs=3))
        cw_grouped_pool = ctx.enter_context(tc.tile_pool(name="cw_grouped", bufs=2))
        eo_grouped_pool = ctx.enter_context(tc.tile_pool(name="eo_grouped", bufs=2))
        result_pool = ctx.enter_context(tc.tile_pool(name="result", bufs=8))
        psum = ctx.enter_context(tc.psum_pool(name="psum", bufs=1))

        def bank(index, shape, dtype):
            tag = "bank%d" % index
            return psum.tile(shape, dtype, name=tag, tag=tag)

        def unit_bank(g, mc):
            return mc * G + g

        identity_f32 = keep.tile([P, P], F32, name="identity_f32")
        make_identity(nc, identity_f32[:])
        identity_bf16 = keep.tile([P, P], BF16, name="identity_bf16")
        make_identity(nc, identity_bf16[:])

        h_words = keep.tile([P, (H_SLOTS + 1) * H_SLOT], U32, name="h_words", align_bytes=64)
        h_scales = keep.tile([P, (H_SLOTS + 1) * H_SLOT], U8, name="h_scales", align_bytes=64)
        cw_words = keep.tile([P, G * S_TILES * HALVES * P], U32, name="cw_words", align_bytes=64)
        cw_scales = keep.tile([P, G * S_TILES * HALVES * P], U8, name="cw_scales", align_bytes=64)
        eo_words = keep.tile([P, HALVES * G * M], U32, name="eo_words", align_bytes=64)
        eo_scales = keep.tile([P, HALVES * G * M], U8, name="eo_scales", align_bytes=64)

        nc.vector.memset(
            h_words[:].bitcast(I32).rearrange("p (slot w) -> p slot w", w=H_SLOT)[:, :, :C], 0
        )
        nc.vector.memset(
            h_scales[:].bitcast(I32).rearrange("p (slot w) -> p slot w", w=H_SLOT // 4)[
                :, :, : C // 4
            ],
            0,
        )

        def h_slot(pair, g, kp):
            return ((pair * G + g) * H_PASSES + kp) * H_SLOT

        h_kept = {}
        h_flipped = {}
        h_grouped_kept = {}

        def load_h(pair):
            h_raw = h_raw_pool.tile([P, 2 * H], BF16)
            nc.sync.dma_start(
                out=h_raw[:].rearrange("p (e k) -> p e k", e=2),
                in_=h[2 * pair : 2 * pair + 2].rearrange("e g c k -> (g c) e k"),
            )
            h_kept[pair] = h_raw

        def transpose_h(pair):
            h_as_words = h_kept[pair][:].bitcast(F32).rearrange(
                "p (e kp w u) -> p e kp u w", e=2, kp=H_PASSES, u=2
            )
            for odd in range(2):
                first_bank = 6 if pair < PAIRS // 2 + 1 else 4
                flipped = bank(first_bank + odd, [P, H_PASSES, 2, P], F32)
                h_flipped[(pair, odd)] = flipped
                for kp in range(H_PASSES):
                    for u in range(2):
                        nc.tensor.transpose(
                            flipped[:, kp, u, :], h_as_words[:, odd, kp, u, :], identity_f32[:]
                        )

        def copy_h(pair):
            h_grouped = grouped_pool.tile([P, H_PASSES * G * 2 * C * PACK], BF16, align_bytes=64)
            h_grouped_kept[pair] = h_grouped
            h_grouped_words = h_grouped[:].bitcast(F32).rearrange(
                "p (kp g o c u) -> p kp g o c u", kp=H_PASSES, g=G, o=2, u=2
            )
            for odd in range(2):
                nc.scalar.copy(
                    out=h_grouped_words[:, :, :, 1 - odd, :, :],
                    in_=h_flipped[(pair, odd)][:].rearrange("p kp u (g c) -> p kp g c u", g=G),
                )

        def quantise_h(pair):
            h_grouped = h_grouped_kept[pair]
            for kp in range(H_PASSES):
                for g in range(G):
                    first = h_slot(pair, g, kp) + C
                    rows = (kp * G + g) * 2 * C * PACK
                    nc.vector.quantize_mx(
                        out=h_words[:, first : first + 2 * C].bitcast(FP8X4),
                        scales=h_scales[:, first : first + 2 * C],
                        in_=h_grouped[:, rows : rows + 2 * C * PACK],
                    )

        cw_raw = {}

        def load_cw(g, q):
            cw_pair = cw_raw_pool.tile([P, 2 * E * C], BF16)
            cw_raw[(g, q)] = cw_pair
            nc.sync.dma_start(
                out=cw_pair[:].rearrange("p (block v) -> p block v", v=CW_RUN),
                in_=combined_weights[g, q * 2 * P : (q + 1) * 2 * P].rearrange(
                    "(block i) (r x) c -> (i r) block (x c)", i=CW_TOKENS, r=E * C // CW_RUN
                ),
            )

        cw_grouped_now = {}

        cw_flipped = {}

        def transpose_cw(g, st):
            flipped = bank(6 + st % 2, [P, CW_BLOCKS, 2, P], BF16)
            cw_flipped[(g, st)] = flipped
            for block in range(CW_BLOCKS):
                for b in range(2):
                    first = (st % 2 * CW_BLOCKS + block) * CW_RUN + b * P
                    nc.tensor.transpose(
                        flipped[:, block, b, :], cw_raw[(g, st // 2)][:, first : first + P], identity_bf16[:]
                    )

        def copy_cw(g, st):
            if st % 2 == 0:
                cw_grouped = cw_grouped_pool.tile([P, 2 * HALVES * P * PACK], BF16, align_bytes=64)
                cw_grouped_now[(g, st // 2)] = cw_grouped
            values = (st % 2) * HALVES * K_PASS
            nc.scalar.copy(
                out=cw_grouped_now[(g, st // 2)][:, values : values + HALVES * K_PASS].bitcast(F32).rearrange(
                    "p (half block i b) -> p half block i b", half=HALVES, block=CW_BLOCKS, b=2
                ),
                in_=cw_flipped[(g, st)][:].rearrange("p block b w -> p (block b w)").bitcast(F32).rearrange(
                    "p (block b i half) -> p half block i b", block=CW_BLOCKS, b=2, half=HALVES
                ),
            )

        def quantise_cw(g, st):
            if st % 2 == 1:
                first = (g * S_TILES + st - 1) * HALVES * P
                nc.vector.quantize_mx(
                    out=cw_words[:, first : first + 2 * HALVES * P].bitcast(FP8X4),
                    scales=cw_scales[:, first : first + 2 * HALVES * P],
                    in_=cw_grouped_now[(g, st // 2)][:],
                )

        wo_mx = {}

        wo_grouped_kept = {}
        wo_kept = {}

        def regroup_wo(e, banks):
            wo_grouped = wo_grouped_pool.tile([P, H_PASSES * M * PACK], BF16, align_bytes=64)
            wo_grouped_kept[e] = wo_grouped
            rows = wo_kept[e][:].rearrange("p kp (j c i) -> p kp c j i", j=PACK, i=4)
            columns = wo_grouped[:].rearrange("p (kp c i j) -> p kp c j i", kp=H_PASSES, i=4, j=PACK)
            if banks == 0:
                nc.vector.tensor_copy(out=columns[:, 0], in_=rows[:, 0])
                nc.scalar.copy(out=columns[:, 1], in_=rows[:, 1])
            else:
                share = COLUMN_GROUPS // 2 + VECTOR_GROUPS_A_BANK * banks
                nc.vector.tensor_copy(out=columns[:, :, :share], in_=rows[:, :, :share])
                nc.scalar.copy(out=columns[:, :, share:], in_=rows[:, :, share:])

        def quantise_wo(e):
            wo_words = wo_mx_pool.tile([P, H_PASSES * M], U32, align_bytes=64)
            wo_scales = wo_mx_pool.tile([P, H_PASSES * M], U8, align_bytes=64)
            wo_mx[e] = (wo_words, wo_scales)
            nc.vector.quantize_mx(
                out=wo_words[:].bitcast(FP8X4), scales=wo_scales[:], in_=wo_grouped_kept[e][:]
            )

        def load_wo(e):
            wo_raw = wo_raw_pool.tile([P, H_PASSES, PACK * M], BF16)
            wo_kept[e] = wo_raw
            rows = wo[e].rearrange("(kp p j) m -> p kp (j m)", kp=H_PASSES, j=PACK)
            if e < WO_LOADS_AHEAD:
                for kp in range(H_PASSES):
                    nc.sync.dma_start(out=wo_raw[:, kp, :], in_=rows[:, kp, :])
            else:
                nc.sync.dma_start(out=wo_raw[:], in_=rows)

        def regroup_wo_columns(e, ch):
            wo_grouped = wo_grouped_pool.tile([P, H_PASSES * HALF_M * PACK], BF16, align_bytes=64)
            wo_grouped_kept[(e, ch)] = wo_grouped
            groups = HALF_M // 4
            for kp in range(H_PASSES):
                rows = wo_kept[e][:, kp, :].rearrange("p (j c i) -> p c j i", j=PACK, i=4)
                columns = wo_grouped[:, kp * HALF_M * PACK : (kp + 1) * HALF_M * PACK].rearrange(
                    "p (c i j) -> p c j i", i=4, j=PACK
                )
                copy_out(nc, kp == 0, out=columns, in_=rows[:, ch * groups : (ch + 1) * groups])

        def quantise_wo_columns(e, ch):
            wo_words = wo_mx_cols_pool.tile([P, H_PASSES * HALF_M], U32, align_bytes=64)
            wo_scales = wo_mx_cols_pool.tile([P, H_PASSES * HALF_M], U8, align_bytes=64)
            wo_mx[(e, ch)] = (wo_words, wo_scales)
            nc.vector.quantize_mx(
                out=wo_words[:].bitcast(FP8X4), scales=wo_scales[:], in_=wo_grouped_kept[(e, ch)][:]
            )

        eo_banks = {}

        def word_place(pair_of_half):
            return 2 * (pair_of_half % 2) + pair_of_half // 2

        def first_product_columns(e, ch):
            t = word_place((e % HALF_EXPERTS) // 2)
            odd = e % 2
            wo_words, wo_scales = wo_mx[(e, ch)]
            for g in range(G):
                for kp in range(H_PASSES):
                    window = h_slot(e // 2, g, kp) + (1 - odd) * 2 * C
                    for c2 in range(HALF_CHUNKS):
                        cols = kp * HALF_M + c2 * M_CHUNK
                        nc.tensor.matmul_mx(
                            out=eo_banks[(g, ch * HALF_CHUNKS + c2)][:, t, :],
                            lhsT=h_words[:, window : window + P].bitcast(FP8X4),
                            lhsT_scale=h_scales[:, window : window + P],
                            rhs=wo_words[:, cols : cols + M_CHUNK].bitcast(FP8X4),
                            rhs_scale=wo_scales[:, cols : cols + M_CHUNK],
                            start=(odd == 0 and kp == 0),
                            stop=(odd == 1 and kp == H_PASSES - 1),
                        )

        def first_product(e, chunks):
            t = word_place((e % HALF_EXPERTS) // 2)
            odd = e % 2
            if e % HALF_EXPERTS == 0:
                for mc in chunks:
                    for g in range(G):
                        eo_banks[(g, mc)] = bank(unit_bank(g, mc), [P, PACK, M_CHUNK], F32)
            wo_words, wo_scales = wo_mx[e]
            for kp in range(H_PASSES):
                for g in range(G):
                    window = h_slot(e // 2, g, kp) + (1 - odd) * 2 * C
                    for mc in chunks:
                        cols = kp * M + mc * M_CHUNK
                        nc.tensor.matmul_mx(
                            out=eo_banks[(g, mc)][:, t, :],
                            lhsT=h_words[:, window : window + P].bitcast(FP8X4),
                            lhsT_scale=h_scales[:, window : window + P],
                            rhs=wo_words[:, cols : cols + M_CHUNK].bitcast(FP8X4),
                            rhs_scale=wo_scales[:, cols : cols + M_CHUNK],
                            start=(odd == 0 and kp == 0),
                            stop=(odd == 1 and kp == H_PASSES - 1),
                        )

        eo_grouped_first = {}

        def copy_first_eo():
            for g in range(G):
                eo_grouped = eo_grouped_pool.tile([P, M * PACK], BF16, align_bytes=64)
                eo_grouped_first[g] = eo_grouped
            for mc in range(M_CHUNKS):
                for g in range(G):
                    out = eo_grouped_first[g][:, mc * K_PASS : (mc + 1) * K_PASS].rearrange(
                        "p (m t) -> p m t", t=PACK
                    )
                    in_ = eo_banks[(g, mc)][:].rearrange("p t m -> p m t")
                    nc.scalar.copy(out=out, in_=in_)

        def quantise_first_eo():
            for g in range(G):
                nc.vector.quantize_mx(
                    out=eo_words[:, g * M : (g + 1) * M].bitcast(FP8X4),
                    scales=eo_scales[:, g * M : (g + 1) * M],
                    in_=eo_grouped_first[g][:],
                )

        def cw_tiles(j):
            return [(j // 2, 2 * (j % 2) + x) for x in range(2)]

        def load_step(r):
            load_wo(r)
            for pair in range(PAIRS):
                if H_STEP[pair] == r:
                    load_h(pair)
            for j in range(len(CW_STEP)):
                if CW_STEP[j] == r:
                    load_cw(j // 2, j % 2)

        def banks_emptied(r):
            return 2 * (H_STEP.count(r) + CW_STEP.count(r)) + (G * M_CHUNKS if r == EO_STEP else 0)

        def transpose_step(r):
            for pair in range(PAIRS):
                if H_STEP[pair] == r:
                    transpose_h(pair)
            for j in range(len(CW_STEP)):
                if CW_STEP[j] == r:
                    for g, st in cw_tiles(j):
                        transpose_cw(g, st)

        def copy_step(r):
            for pair in range(PAIRS):
                if H_STEP[pair] == r:
                    copy_h(pair)
            for j in range(len(CW_STEP)):
                if CW_STEP[j] == r:
                    for g, st in cw_tiles(j):
                        copy_cw(g, st)

        def quantise_step(r):
            for pair in range(PAIRS):
                if H_STEP[pair] == r:
                    quantise_h(pair)
            for j in range(len(CW_STEP)):
                if CW_STEP[j] == r:
                    quantise_cw(j // 2, 2 * (j % 2) + 1)
            quantise_wo(r)

        multiplied = {}

        def multiply_step(r):
            def multiply_waiting(half, chunks, first_step, experts):
                for e in experts:
                    if e == multiplied.get((half, chunks), half * HALF_EXPERTS) and H_STEP[e // 2] <= r >= first_step:
                        first_product(e, chunks)
                        multiplied[(half, chunks)] = e + 1

            for half in range(HALVES):
                experts = range(half * HALF_EXPERTS, min(r + 1, (half + 1) * HALF_EXPERTS))
                if half == 1:
                    for chunks, first_step in CHUNK_STEPS[half]:
                        multiply_waiting(half, chunks, first_step, experts[:-1])
                for chunks, first_step in CHUNK_STEPS[half]:
                    multiply_waiting(half, chunks, first_step, experts)

        out_rows = out.rearrange("g (st i) m -> i g st m", st=S_TILES)
        eo_grouped_columns = {}
        accs = {}

        def vector_empties(ch, g, i):
            return i == 0 and not (ch == 0 and g == 0)

        def copy_eo_columns(ch):
            for g in range(G):
                eo_grouped = eo_grouped_pool.tile([P, M * PACK], BF16, align_bytes=64)
                eo_grouped_columns[(ch, g)] = eo_grouped
                for c2 in range(HALF_CHUNKS):
                    copy_out(
                        nc,
                        vector_empties(ch, g, c2),
                        out=eo_grouped[:, c2 * K_PASS : (c2 + 1) * K_PASS].rearrange(
                            "p (m t) -> p m t", t=PACK
                        ),
                        in_=eo_banks[(g, ch * HALF_CHUNKS + c2)][:].rearrange("p t m -> p m t"),
                    )

        def quantise_eo_columns(ch):
            for g in range(G):
                first = (G + g) * M + ch * HALF_M
                nc.vector.quantize_mx(
                    out=eo_words[:, first : first + HALF_M].bitcast(FP8X4),
                    scales=eo_scales[:, first : first + HALF_M],
                    in_=eo_grouped_columns[(ch, g)][:, : HALF_M * PACK],
                )

        def second_product_columns(ch):
            for g in range(G):
                for q in range(S_TILES // 2):
                    acc = bank(unit_bank(g, ch * HALF_CHUNKS + q), [P, 2, HALF_M], F32)
                    accs[(ch, g, q)] = acc
                    for s2 in range(2):
                        st = 2 * q + s2
                        for half in range(HALVES):
                            tokens = ((g * S_TILES + st) * HALVES + half) * P
                            cols = (half * G + g) * M + ch * HALF_M
                            nc.tensor.matmul_mx(
                                out=acc[:, s2, :],
                                lhsT=cw_words[:, tokens : tokens + P].bitcast(FP8X4),
                                lhsT_scale=cw_scales[:, tokens : tokens + P],
                                rhs=eo_words[:, cols : cols + HALF_M].bitcast(FP8X4),
                                rhs_scale=eo_scales[:, cols : cols + HALF_M],
                                start=(half == 0),
                                stop=(half == HALVES - 1),
                            )

        def store_columns(ch):
            for g in range(G):
                for q in range(S_TILES // 2):
                    result = result_pool.tile([P, 2, HALF_M], F32)
                    copy_out(nc, vector_empties(ch, g, q), out=result[:], in_=accs[(ch, g, q)][:])
                    nc.sync.dma_start(
                        out=out_rows[:, g, 2 * q : 2 * q + 2, ch * HALF_M : (ch + 1) * HALF_M], in_=result[:]
                    )

        with tc.manual_schedule():
            for r in range(WHOLE_EXPERTS):
                load_step(r)
                transpose_step(r)
                regroup_wo(r, banks_emptied(r))
                copy_step(r)
                if r > 0:
                    quantise_step(r - 1)
                if r == EO_STEP:
                    copy_first_eo()
                if r == EO_STEP + 1:
                    quantise_first_eo()
                if r > 0:
                    multiply_step(r - 1)
            for e in range(WHOLE_EXPERTS, E):
                load_wo(e)

            regroup_wo_columns(WHOLE_EXPERTS, 0)
            quantise_step(WHOLE_EXPERTS - 1)
            multiply_step(WHOLE_EXPERTS - 1)
            pieces = [(e, ch) for ch in range(COLUMN_HALVES) for e in range(WHOLE_EXPERTS, E)]
            for i in range(len(pieces)):
                if i + 1 < len(pieces):
                    regroup_wo_columns(pieces[i + 1][0], pieces[i + 1][1])
                quantise_wo_columns(pieces[i][0], pieces[i][1])
                first_product_columns(pieces[i][0], pieces[i][1])
            copy_eo_columns(0)
            quantise_eo_columns(0)
            second_product_columns(0)
            copy_eo_columns(1)
            quantise_eo_columns(1)
            second_product_columns(1)
            store_columns(0)
            store_columns(1)
